import numpy as np
import ml_dtypes


def mxq(x, axis, fmt="e4m3"):
    dtype, down = {"e4m3": (ml_dtypes.float8_e4m3fn, 7), "e5m2": (ml_dtypes.float8_e5m2, 14)}[fmt]
    v = np.moveaxis(np.asarray(x, np.float32).astype(ml_dtypes.bfloat16).astype(np.float64), axis, -1)
    blocks = v.reshape(v.shape[:-1] + (-1, 32))
    amax = np.abs(blocks).max(-1, keepdims=True)
    byte = np.maximum(np.where(amax > 0, np.frexp(amax)[1] - 1 + 127, 0) - down, 1)
    scale = np.exp2(byte - 127.0)
    codes = (blocks / scale).astype(np.float32).astype(dtype).astype(np.float64)
    return np.moveaxis((codes * scale).reshape(v.shape), -1, axis)


WIDE = False


def mx_kscale(k):
    if not WIDE:
        return np.ones(k)
    levels = np.array([10, -10, 5, -5, 0])
    a = np.random.permutation(np.resize(levels, k // 512 * 4)).reshape(k // 512, 4)
    idx = np.arange(k)
    return np.exp2(a[idx // 512, idx % 128 // 32])


BF16 = ml_dtypes.bfloat16


def bf(x):
    return np.asarray(x, np.float32).astype(BF16)


def f64(x):
    return np.asarray(x).astype(np.float64)


E2M1 = np.array([0.0, 0.5, 1.0, 1.5, 2.0, 3.0, 4.0, 6.0, -0.0, -0.5, -1.0, -1.5, -2.0, -3.0, -4.0, -6.0])


def pack_weight(w, fmt):
    k, n = w.shape
    w = f64(bf(w)).reshape(k // 32, 32, n)
    amax = np.abs(w).max(1)
    if fmt == "e4m3":
        byte = np.frexp(amax)[1] - 1 + 127 - 7
    else:
        mant, ex = np.frexp(amax / 6.0)
        byte = np.where(mant > 0.5, ex, ex - 1) + 127
    byte = np.clip(np.where(amax > 0, byte, 1), 1, 254)
    scaled = (w * np.exp2(127.0 - byte)[:, None, :]).reshape(k, n).astype(np.float32)
    by_word = np.ascontiguousarray(scaled.reshape(k // 512, 128, 4, n).transpose(0, 1, 3, 2))
    if fmt == "e4m3":
        words = by_word.astype(ml_dtypes.float8_e4m3fn).view(np.uint8)
    else:
        c = by_word.astype(ml_dtypes.float4_e2m1fn).view(np.uint8) & 0xF
        words = c[..., 0::2] | (c[..., 1::2] << 4)
    return np.ascontiguousarray(words), np.ascontiguousarray(byte.astype(np.uint8).reshape(k // 512, 16, n))


def unpack_weight(words, scales, fmt):
    g, p, n, _ = words.shape
    if fmt == "e4m3":
        vals = np.ascontiguousarray(words).view(ml_dtypes.float8_e4m3fn).astype(np.float64)
    else:
        nib = np.empty((g, p, n, 4), np.uint8)
        nib[..., 0::2] = words & 0xF
        nib[..., 1::2] = words >> 4
        vals = E2M1[nib]
    vals = vals * np.repeat(np.exp2(scales.astype(np.float64) - 127.0), 8, axis=1)[..., None]
    return vals.transpose(0, 1, 3, 2).reshape(g * 512, n)


BATCH, IN_FEATURES, OUT_FEATURES, LOG_DIM = 512, 2048, 2048, 11
BUTTERFLY_DIM = 2 ** LOG_DIM
MAX_BLOCKS = BUTTERFLY_DIM // 2
FMT = "e4m3"


def setup_inputs():
    s = mx_kscale(IN_FEATURES)
    x = np.random.standard_normal((BATCH, IN_FEATURES)) * s
    w_in = np.random.standard_normal((BUTTERFLY_DIM, IN_FEATURES)) / np.sqrt(IN_FEATURES) / s[None, :]
    w_out = np.random.standard_normal((OUT_FEATURES, BUTTERFLY_DIM)) / np.sqrt(BUTTERFLY_DIM)
    b_out = np.random.standard_normal(OUT_FEATURES) * 0.1
    theta = np.random.uniform(0.0, 1.0, (LOG_DIM, MAX_BLOCKS))
    w_in_words, w_in_scales = pack_weight(np.ascontiguousarray(w_in.T), FMT)
    w_out_words, w_out_scales = pack_weight(np.ascontiguousarray(w_out.T), FMT)
    return {"x": bf(x), "w_in_words": w_in_words, "w_in_scales": w_in_scales,
            "w_out_words": w_out_words, "w_out_scales": w_out_scales, "b_out": bf(b_out),
            "a_pad": bf(np.cos(theta)), "b_pad": bf(np.sin(theta))}


def _butterfly(x, a_pad, b_pad):
    B = x.shape[0]
    for l in range(LOG_DIM):
        block_size = 2 ** l
        num_blocks = BUTTERFLY_DIM // (2 * block_size)
        a = a_pad[l, :num_blocks][None, :, None]
        b = b_pad[l, :num_blocks][None, :, None]
        xv = x.reshape(B, num_blocks, 2, block_size)
        x0 = xv[:, :, 0, :]
        x1 = xv[:, :, 1, :]
        top = a * x0 + b * x1
        bot = -b * x0 + a * x1
        x = np.stack([top, bot], axis=2).reshape(B, BUTTERFLY_DIM)
    return x


def reference(x, w_in_words, w_in_scales, w_out_words, w_out_scales, b_out, a_pad, b_pad):
    h = mxq(f64(x), 1, "e4m3") @ unpack_weight(w_in_words, w_in_scales, FMT)
    h = _butterfly(h, f64(a_pad), f64(b_pad))
    return (mxq(h, 1, "e4m3") @ unpack_weight(w_out_words, w_out_scales, FMT)) + f64(b_out)

@@ -1,0 +1,329 @@
+from contextlib import ExitStack
+
+import concourse.mybir as mybir
+from concourse.masks import make_identity
+
+F32 = mybir.dt.float32
+BF16 = mybir.dt.bfloat16
+I32 = mybir.dt.int32
+U8 = mybir.dt.uint8
+FP8X4 = mybir.dt.float8_e4m3fn_x4
+MULT = mybir.AluOpType.mult
+ADD = mybir.AluOpType.add
+
+P = 128
+BATCH = 512
+FEATURES = 2048
+PACK = 4
+PASSES = FEATURES // (P * PACK)
+HALVES = 2
+HALF = BATCH // HALVES
+TREES = FEATURES // P
+LEVELS = 11
+LOW_LEVELS = 7
+MAX_BLOCKS = FEATURES // 2
+B_ROW = 64
+HIGH_ROW = 32
+HIGH_BIT = 3
+BANK = 512
+
+FLOPS = 2 * 2 * BATCH * FEATURES * FEATURES + 3 * LEVELS * BATCH * FEATURES
+
+
+def tile_butterflylayer_kernel(
+    tc, x, w_in_words, w_in_scales, w_out_words, w_out_scales, b_out, a_pad, b_pad, out
+):
+    nc = tc.nc
+
+    def copy_out(index, dst, src):
+        if index % 2 == 0:
+            nc.scalar.copy(out=dst, in_=src)
+        else:
+            nc.vector.tensor_copy(out=dst, in_=src)
+
+    with ExitStack() as stack:
+        stack.enter_context(tc.manual_schedule())
+        keep = stack.enter_context(tc.tile_pool(name="keep", bufs=1))
+        psum = stack.enter_context(tc.psum_pool(name="psum", bufs=4))
+
+        w_in_sb = keep.tile([P, PASSES, FEATURES], I32, align_bytes=64)
+        w_out_sb = keep.tile([P, PASSES, FEATURES], I32, align_bytes=64)
+        w_in_planes = keep.tile([P, FEATURES], U8, align_bytes=64)
+        w_out_planes = keep.tile([P, FEATURES], U8, align_bytes=64)
+        x_codes = keep.tile([P, HALVES, PASSES, HALF], I32, align_bytes=64)
+        x_planes = keep.tile([P, HALVES, PASSES, HALF], U8, align_bytes=64)
+        h_codes = keep.tile([P, HALVES, PASSES, HALF], I32, align_bytes=64)
+        h_planes = keep.tile([P, HALVES, PASSES, HALF], U8, align_bytes=64)
+        h_sb = keep.tile([P, HALVES, TREES, HALF], F32)
+        rot = keep.tile([P, TREES + 1, P], F32)
+        rot_t = keep.tile([P, TREES + 1, P], F32)
+        ident = keep.tile([P, P], F32)
+        bias_sb = keep.tile([P, FEATURES], BF16)
+
+        with tc.tile_pool(name="early", bufs=1) as early, tc.psum_pool(name="tables", bufs=1) as tables:
+            x_sb = early.tile([P, BATCH // P, FEATURES], BF16)
+            coeff = early.tile([P, MAX_BLOCKS + 16], BF16)
+
+            nc.vector.memset(w_in_planes[:].bitcast(I32), 0)
+            nc.vector.memset(coeff[:].bitcast(I32), 0)
+            nc.vector.memset(w_out_planes[:].bitcast(I32), 0)
+            make_identity(nc, ident[:])
+
+            high_blocks = MAX_BLOCKS >> LOW_LEVELS
+            for row, table in ((0, a_pad), (B_ROW, b_pad)):
+                nc.scalar.dma_start(out=coeff[row : row + LOW_LEVELS, 0:MAX_BLOCKS], in_=table[0:LOW_LEVELS, :])
+                nc.scalar.dma_start(
+                    out=coeff[
+                        row + HIGH_ROW + HIGH_BIT : row + HIGH_ROW + HIGH_BIT + LEVELS - LOW_LEVELS,
+                        MAX_BLOCKS : MAX_BLOCKS + high_blocks,
+                    ],
+                    in_=table[LOW_LEVELS:LEVELS, 0:high_blocks],
+                )
+
+            def load_x(half):
+                for rows in range(half * (HALF // P), (half + 1) * (HALF // P)):
+                    nc.sync.dma_start(out=x_sb[:, rows, :], in_=x[P * rows : P * (rows + 1), :])
+
+            w_in_scale_words = w_in_scales.bitcast(I32)
+            for quadrant in range(4):
+                nc.sync.dma_start(
+                    out=w_in_planes[32 * quadrant : 32 * quadrant + 16, :].bitcast(I32),
+                    in_=w_in_scale_words[:, 4 * quadrant : 4 * quadrant + 4, :],
+                )
+            load_x(0)
+            w_in_view = w_in_words.rearrange("g p n t -> g p (n t)").bitcast(I32).rearrange("g p n -> p g n")
+            for first in range(0, FEATURES, BANK):
+                nc.sync.dma_start(out=w_in_sb[:, :, first : first + BANK], in_=w_in_view[:, :, first : first + BANK])
+            load_x(1)
+            w_out_scale_words = w_out_scales.bitcast(I32)
+            for quadrant in range(4):
+                nc.sync.dma_start(
+                    out=w_out_planes[32 * quadrant : 32 * quadrant + 16, :].bitcast(I32),
+                    in_=w_out_scale_words[quadrant].rearrange("(h c) n -> c h n", c=PASSES),
+                )
+            w_out_view = (
+                w_out_words.rearrange("g p n t -> g p (n t)")
+                .bitcast(I32)
+                .rearrange("g (h c r) n -> c (g h) r n", h=4, c=PASSES, r=8)
+            )
+            for c in range(PASSES):
+                nc.sync.dma_start(out=w_out_sb[:, c, :], in_=w_out_view[c])
+            nc.sync.dma_start(out=bias_sb[:], in_=b_out.partition_broadcast(P))
+
+            pick = early.tile([P, 2, LOW_LEVELS, P], BF16)
+            nc.vector.memset(pick[:].rearrange("k e l i -> k (e l i)").bitcast(I32), 0)
+            for bit in range(LOW_LEVELS):
+                for e in range(2):
+                    by_bit = pick[:, e, bit, :].rearrange("k (hi t lo) -> k hi t lo", t=2, lo=2**bit)
+                    nc.vector.memset(by_bit[0:B_ROW, :, e, :], 1.0)
+                    nc.vector.memset(by_bit[B_ROW:P, :, 1 - e, :], 2.0 * e - 1.0)
+            own_bit_f32 = early.tile([P, LOW_LEVELS], F32)
+            nc.vector.tensor_reduce(
+                out=own_bit_f32[:],
+                in_=ident[:].rearrange("k (q l) -> k l q", l=HIGH_ROW)[:, 0:LOW_LEVELS, :],
+                axis=mybir.AxisListType.X,
+                op=ADD,
+            )
+            own_bit = early.tile([P, LOW_LEVELS], BF16)
+            nc.vector.tensor_copy(out=own_bit[:], in_=own_bit_f32[:])
+            nc.vector.tensor_tensor(
+                out=pick[:],
+                in0=pick[:],
+                in1=own_bit[:].unsqueeze(1).unsqueeze(3).to_broadcast([P, 2, LOW_LEVELS, P]),
+                op=MULT,
+            )
+
+            factor = [tables.tile([P, 2, BANK], BF16, name="factor%d" % bank) for bank in range(4)]
+
+            def factor_part(stage, start, width):
+                column = FEATURES - (FEATURES >> stage) + start
+                return factor[column // BANK][:, :, column % BANK : column % BANK + width]
+
+            def rotation_factors():
+                for stage in range(LEVELS):
+                    blocks = MAX_BLOCKS >> stage
+                    bit = stage if stage < LOW_LEVELS else stage - LOW_LEVELS + HIGH_BIT
+                    first_column = 0 if stage < LOW_LEVELS else MAX_BLOCKS
+                    width = min(blocks, BANK)
+                    for start in range(0, blocks, width):
+                        for e in range(2):
+                            nc.tensor.matmul(
+                                out=factor_part(stage, start, width)[:, e, :],
+                                lhsT=pick[:, e, bit, :],
+                                rhs=coeff[:, first_column + start : first_column + start + width],
+                                start=True,
+                                stop=True,
+                            )
+
+            def rotation_products(first, end, result):
+                old = None
+                for stage in reversed(range(first, end)):
+                    blocks = MAX_BLOCKS >> stage
+                    new = result if stage == first else early.tile([P, 2 * blocks], F32, name="product%d" % stage)
+                    width = min(blocks, BANK)
+                    for start in range(0, blocks, width):
+                        new_part = new[:, 2 * start : 2 * (start + width)].rearrange("p (b e) -> p b e", e=2)
+                        by_block = factor_part(stage, start, width).rearrange("p e b -> p b e")
+                        if old is None:
+                            nc.vector.tensor_copy(out=new_part, in_=by_block)
+                        else:
+                            nc.vector.tensor_tensor(
+                                out=new_part,
+                                in0=old[:, start : start + width].unsqueeze(2).to_broadcast([P, width, 2]),
+                                in1=by_block,
+                                op=MULT,
+                            )
+                    old = new
+
+            def rotation_matrices():
+                rotation_products(0, LOW_LEVELS, rot[:, 0:TREES, :].rearrange("p s j -> p (s j)"))
+                high = early.tile([P, TREES], F32)
+                rotation_products(LOW_LEVELS, LEVELS, high[:])
+                same_r = early.tile([P, 8], F32)
+                nc.vector.tensor_reduce(
+                    out=same_r[:], in_=ident[:].rearrange("p (h r) -> p r h", r=8), axis=mybir.AxisListType.X, op=ADD
+                )
+                nc.vector.tensor_tensor(
+                    out=rot[:, TREES, :].rearrange("p (h r) -> p h r", r=8),
+                    in0=high[:].unsqueeze(2).to_broadcast([P, TREES, 8]),
+                    in1=same_r[:].unsqueeze(1).to_broadcast([P, TREES, 8]),
+                    op=MULT,
+                )
+
+            def quantise_x(half):
+                grouped = []
+                for g in range(PASSES):
+                    x_t = psum.tile([P, 2, HALF], F32, tag="bank")
+                    for u in range(2):
+                        for rows in range(HALF // P):
+                            x_words = x_sb[:, half * (HALF // P) + rows, :].bitcast(F32)
+                            nc.tensor.transpose(
+                                out=x_t[:, u, P * rows : P * (rows + 1)],
+                                in_=x_words[:, 256 * g + u : 256 * (g + 1) : 2],
+                                identity=ident[:],
+                            )
+                    x_grouped = early.tile([P, HALF, PACK], BF16, align_bytes=64, bufs=PASSES)
+                    copy_out(
+                        g,
+                        x_grouped[:].rearrange("p b t -> p (b t)").bitcast(F32).rearrange("p (b u) -> p b u", u=2),
+                        x_t[:].rearrange("p u b -> p b u"),
+                    )
+                    grouped.append(x_grouped)
+                for g in range(PASSES):
+                    nc.vector.quantize_mx(
+                        out=x_codes[:, half, g, :].bitcast(FP8X4),
+                        scales=x_planes[:, half, g, :],
+                        in_=grouped[g][:].rearrange("p b t -> p (b t)"),
+                    )
+
+            def first_linear_map(half):
+                for pair in range(TREES // 2):
+                    acc = psum.tile([P, 2, HALF], F32, tag="bank")
+                    for i in range(2):
+                        cols = slice(P * (2 * pair + i), P * (2 * pair + i + 1))
+                        for g in range(PASSES):
+                            nc.tensor.matmul_mx(
+                                out=acc[:, i, :],
+                                lhsT=w_in_sb[:, g, cols].bitcast(FP8X4),
+                                lhsT_scale=w_in_planes[PACK * g : P, cols],
+                                rhs=x_codes[:, half, g, :].bitcast(FP8X4),
+                                rhs_scale=x_planes[:, half, g, :],
+                                start=(g == 0),
+                                stop=(g == PASSES - 1),
+                            )
+                    nc.scalar.copy(out=h_sb[:, half, 2 * pair : 2 * pair + 2, :], in_=acc[:])
+
+            def transpose_rotations():
+                for first in range(0, TREES + 1, 4):
+                    n = min(4, TREES + 1 - first)
+                    flipped = psum.tile([P, 4, P], F32, tag="bank")
+                    for i in range(n):
+                        nc.tensor.transpose(out=flipped[:, i, :], in_=rot[:, first + i, :], identity=ident[:])
+                    copy_out(first // 4, rot_t[:, first : first + n, :], flipped[:, 0:n, :])
+
+            quantise_x(0)
+            rotation_factors()
+            rotation_matrices()
+            first_linear_map(0)
+            quantise_x(1)
+            transpose_rotations()
+            first_linear_map(1)
+
+        with tc.tile_pool(name="late", bufs=1) as late:
+            parked = [
+                out[HALF * half : HALF * (half + 1), :].rearrange("r (f b) -> (r f) b", b=HALF)
+                for half in range(HALVES)
+            ]
+            back = []
+            for half in range(HALVES):
+                for four in range(TREES // 4):
+                    low = late.tile([P, 4, HALF], F32, bufs=4)
+                    for pair in range(2):
+                        acc = psum.tile([P, 2, HALF], F32, tag="bank")
+                        for i in range(2):
+                            tree = 4 * four + 2 * pair + i
+                            nc.tensor.matmul(
+                                out=acc[:, i, :],
+                                lhsT=rot_t[:, tree, :],
+                                rhs=h_sb[:, half, tree, :],
+                                start=True,
+                                stop=True,
+                            )
+                        copy_out(pair, low[:, 2 * pair : 2 * pair + 2, :], acc[:])
+                    nc.sync.dma_start(
+                        out=parked[half].rearrange("(s l) b -> l s b", l=P)[:, 4 * four : 4 * four + 4, :],
+                        in_=low[:],
+                    )
+                returned = late.tile([P, PASSES, PACK, HALF], F32, bufs=HALVES)
+                by_pass = parked[half].rearrange("(h c r t) b -> c h r (t b)", h=TREES, c=PASSES, r=8, t=PACK)
+                for c in range(PASSES):
+                    nc.sync.dma_start(out=returned[:, c].rearrange("p t b -> p (t b)"), in_=by_pass[c])
+                back.append(returned)
+
+            for half in range(HALVES):
+                for c in range(PASSES):
+                    grouped = late.tile([P, HALF, PACK], BF16, align_bytes=64, bufs=3)
+                    for rows in range(HALF // P):
+                        acc = psum.tile([P, PACK, P], F32, tag="bank")
+                        nc.tensor.matmul(
+                            out=acc[:],
+                            lhsT=rot_t[:, TREES, :],
+                            rhs=back[half][:, c, :, P * rows : P * (rows + 1)],
+                            start=True,
+                            stop=True,
+                        )
+                        copy_out(rows, grouped[:, P * rows : P * (rows + 1), :], acc[:].rearrange("p t b -> p b t"))
+                    nc.vector.quantize_mx(
+                        out=h_codes[:, half, c, :].bitcast(FP8X4),
+                        scales=h_planes[:, half, c, :],
+                        in_=grouped[:].rearrange("p b t -> p (b t)"),
+                    )
+
+            for half in range(HALVES):
+                for rows in range(HALF // P):
+                    batch = slice(P * rows, P * (rows + 1))
+                    for wide in range(FEATURES // (2 * BANK)):
+                        result = late.tile([P, 2 * BANK], F32, bufs=3)
+                        for i in range(2):
+                            cols = slice(BANK * (2 * wide + i), BANK * (2 * wide + i + 1))
+                            acc = psum.tile([P, BANK], F32, tag="bank")
+                            for c in range(PASSES):
+                                nc.tensor.matmul_mx(
+                                    out=acc[:],
+                                    lhsT=h_codes[:, half, c, batch].bitcast(FP8X4),
+                                    lhsT_scale=h_planes[:, half, c, batch],
+                                    rhs=w_out_sb[:, c, cols].bitcast(FP8X4),
+                                    rhs_scale=w_out_planes[PACK * c : P, cols],
+                                    start=(c == 0),
+                                    stop=(c == PASSES - 1),
+                                )
+                            nc.vector.tensor_tensor(
+                                out=result[:, BANK * i : BANK * (i + 1)], in0=acc[:], in1=bias_sb[:, cols], op=ADD
+                            )
+                        nc.sync.dma_start(
+                            out=out[
+                                HALF * half + P * rows : HALF * half + P * (rows + 1),
+                                2 * BANK * wide : 2 * BANK * (wide + 1),
+                            ],
+                            in_=result[:],
+                        )

@@ -44,7 +44,6 @@ def tile_butterflylayer_kernel(
     with ExitStack() as stack:
         stack.enter_context(tc.manual_schedule())
         keep = stack.enter_context(tc.tile_pool(name="keep", bufs=1))
-        psum = stack.enter_context(tc.psum_pool(name="psum", bufs=4))
 
         w_in_sb = keep.tile([P, PASSES, FEATURES], I32, align_bytes=64)
         w_out_sb = keep.tile([P, PASSES, FEATURES], I32, align_bytes=64)
@@ -60,7 +59,35 @@ def tile_butterflylayer_kernel(
         ident = keep.tile([P, P], F32)
         bias_sb = keep.tile([P, FEATURES], BF16)
 
-        with tc.tile_pool(name="early", bufs=1) as early, tc.psum_pool(name="tables", bufs=1) as tables:
+        def first_linear_map(half, banks):
+            for pair in range(TREES // 2):
+                acc = banks.tile([P, 2, HALF], F32, tag="bank")
+                for i in range(2):
+                    cols = slice(P * (2 * pair + i), P * (2 * pair + i + 1))
+                    for g in range(PASSES):
+                        nc.tensor.matmul_mx(
+                            out=acc[:, i, :],
+                            lhsT=w_in_sb[:, g, cols].bitcast(FP8X4),
+                            lhsT_scale=w_in_planes[PACK * g : P, cols],
+                            rhs=x_codes[:, half, g, :].bitcast(FP8X4),
+                            rhs_scale=x_planes[:, half, g, :],
+                            start=(g == 0),
+                            stop=(g == PASSES - 1),
+                        )
+                nc.scalar.copy(out=h_sb[:, half, 2 * pair : 2 * pair + 2, :], in_=acc[:])
+
+        def transpose_rotations(banks):
+            for first in range(0, TREES + 1, 4):
+                n = min(4, TREES + 1 - first)
+                flipped = banks.tile([P, 4, P], F32, tag="bank")
+                for i in range(n):
+                    nc.tensor.transpose(out=flipped[:, i, :], in_=rot[:, first + i, :], identity=ident[:])
+                copy_out(first // 4, rot_t[:, first : first + n, :], flipped[:, 0:n, :])
+
+
+        with tc.tile_pool(name="early", bufs=1) as early, tc.psum_pool(name="tables", bufs=1) as tables, tc.psum_pool(
+            name="first_banks", bufs=4
+        ) as banks:
             x_sb = early.tile([P, BATCH // P, FEATURES], BF16)
             coeff = early.tile([P, MAX_BLOCKS + 16], BF16)
 
@@ -91,10 +118,10 @@ def tile_butterflylayer_kernel(
                     in_=w_in_scale_words[:, 4 * quadrant : 4 * quadrant + 4, :],
                 )
             load_x(0)
+            load_x(1)
             w_in_view = w_in_words.rearrange("g p n t -> g p (n t)").bitcast(I32).rearrange("g p n -> p g n")
             for first in range(0, FEATURES, BANK):
                 nc.sync.dma_start(out=w_in_sb[:, :, first : first + BANK], in_=w_in_view[:, :, first : first + BANK])
-            load_x(1)
             w_out_scale_words = w_out_scales.bitcast(I32)
             for quadrant in range(4):
                 nc.sync.dma_start(
@@ -193,7 +220,7 @@ def tile_butterflylayer_kernel(
             def quantise_x(half):
                 grouped = []
                 for g in range(PASSES):
-                    x_t = psum.tile([P, 2, HALF], F32, tag="bank")
+                    x_t = banks.tile([P, 2, HALF], F32, tag="bank")
                     for u in range(2):
                         for rows in range(HALF // P):
                             x_words = x_sb[:, half * (HALF // P) + rows, :].bitcast(F32)
@@ -216,50 +243,23 @@ def tile_butterflylayer_kernel(
                         in_=grouped[g][:].rearrange("p b t -> p (b t)"),
                     )
 
-            def first_linear_map(half):
-                for pair in range(TREES // 2):
-                    acc = psum.tile([P, 2, HALF], F32, tag="bank")
-                    for i in range(2):
-                        cols = slice(P * (2 * pair + i), P * (2 * pair + i + 1))
-                        for g in range(PASSES):
-                            nc.tensor.matmul_mx(
-                                out=acc[:, i, :],
-                                lhsT=w_in_sb[:, g, cols].bitcast(FP8X4),
-                                lhsT_scale=w_in_planes[PACK * g : P, cols],
-                                rhs=x_codes[:, half, g, :].bitcast(FP8X4),
-                                rhs_scale=x_planes[:, half, g, :],
-                                start=(g == 0),
-                                stop=(g == PASSES - 1),
-                            )
-                    nc.scalar.copy(out=h_sb[:, half, 2 * pair : 2 * pair + 2, :], in_=acc[:])
-
-            def transpose_rotations():
-                for first in range(0, TREES + 1, 4):
-                    n = min(4, TREES + 1 - first)
-                    flipped = psum.tile([P, 4, P], F32, tag="bank")
-                    for i in range(n):
-                        nc.tensor.transpose(out=flipped[:, i, :], in_=rot[:, first + i, :], identity=ident[:])
-                    copy_out(first // 4, rot_t[:, first : first + n, :], flipped[:, 0:n, :])
 
             quantise_x(0)
+            quantise_x(1)
             rotation_factors()
             rotation_matrices()
-            first_linear_map(0)
-            quantise_x(1)
-            transpose_rotations()
-            first_linear_map(1)
+            first_linear_map(0, banks)
 
-        with tc.tile_pool(name="late", bufs=1) as late:
-            parked = [
-                out[HALF * half : HALF * (half + 1), :].rearrange("r (f b) -> (r f) b", b=HALF)
-                for half in range(HALVES)
-            ]
-            back = []
-            for half in range(HALVES):
+        with tc.tile_pool(name="late", bufs=1, reuse_waits="tile") as late, tc.psum_pool(
+            name="banks", bufs=8, reuse_waits="tile"
+        ) as banks:
+
+            def low_stages(half):
+                parked = out[HALF * half : HALF * (half + 1), :].rearrange("r (f b) -> (r f) b", b=HALF)
                 for four in range(TREES // 4):
                     low = late.tile([P, 4, HALF], F32, bufs=4)
                     for pair in range(2):
-                        acc = psum.tile([P, 2, HALF], F32, tag="bank")
+                        acc = banks.tile([P, 2, HALF], F32, tag="bank")
                         for i in range(2):
                             tree = 4 * four + 2 * pair + i
                             nc.tensor.matmul(
@@ -271,24 +271,23 @@ def tile_butterflylayer_kernel(
                             )
                         copy_out(pair, low[:, 2 * pair : 2 * pair + 2, :], acc[:])
                     nc.sync.dma_start(
-                        out=parked[half].rearrange("(s l) b -> l s b", l=P)[:, 4 * four : 4 * four + 4, :],
-                        in_=low[:],
+                        out=parked.rearrange("(s l) b -> l s b", l=P)[:, 4 * four : 4 * four + 4, :], in_=low[:]
                     )
                 returned = late.tile([P, PASSES, PACK, HALF], F32, bufs=HALVES)
-                by_pass = parked[half].rearrange("(h c r t) b -> c h r (t b)", h=TREES, c=PASSES, r=8, t=PACK)
+                by_pass = parked.rearrange("(h c r t) b -> c h r (t b)", h=TREES, c=PASSES, r=8, t=PACK)
                 for c in range(PASSES):
                     nc.sync.dma_start(out=returned[:, c].rearrange("p t b -> p (t b)"), in_=by_pass[c])
-                back.append(returned)
+                return returned
 
-            for half in range(HALVES):
+            def high_stages(half, returned):
                 for c in range(PASSES):
                     grouped = late.tile([P, HALF, PACK], BF16, align_bytes=64, bufs=3)
                     for rows in range(HALF // P):
-                        acc = psum.tile([P, PACK, P], F32, tag="bank")
+                        acc = banks.tile([P, PACK, P], F32, tag="bank")
                         nc.tensor.matmul(
                             out=acc[:],
                             lhsT=rot_t[:, TREES, :],
-                            rhs=back[half][:, c, :, P * rows : P * (rows + 1)],
+                            rhs=returned[:, c, :, P * rows : P * (rows + 1)],
                             start=True,
                             stop=True,
                         )
@@ -299,14 +298,14 @@ def tile_butterflylayer_kernel(
                         in_=grouped[:].rearrange("p b t -> p (b t)"),
                     )
 
-            for half in range(HALVES):
+            def second_linear_map(half):
                 for rows in range(HALF // P):
                     batch = slice(P * rows, P * (rows + 1))
                     for wide in range(FEATURES // (2 * BANK)):
                         result = late.tile([P, 2 * BANK], F32, bufs=3)
                         for i in range(2):
                             cols = slice(BANK * (2 * wide + i), BANK * (2 * wide + i + 1))
-                            acc = psum.tile([P, BANK], F32, tag="bank")
+                            acc = banks.tile([P, BANK], F32, tag="bank")
                             for c in range(PASSES):
                                 nc.tensor.matmul_mx(
                                     out=acc[:],
@@ -327,3 +326,12 @@ def tile_butterflylayer_kernel(
                             ],
                             in_=result[:],
                         )
+
+            transpose_rotations(banks)
+            returned_0 = low_stages(0)
+            first_linear_map(1, banks)
+            returned_1 = low_stages(1)
+            high_stages(0, returned_0)
+            second_linear_map(0)
+            high_stages(1, returned_1)
+            second_linear_map(1)

@@ -91,10 +91,10 @@ def tile_butterflylayer_kernel(
             x_sb = early.tile([P, BATCH // P, FEATURES], BF16)
             coeff = early.tile([P, MAX_BLOCKS + 16], BF16)
 
-            nc.vector.memset(w_in_planes[:].bitcast(I32), 0)
-            nc.vector.memset(coeff[:].bitcast(I32), 0)
-            nc.vector.memset(w_out_planes[:].bitcast(I32), 0)
+            nc.gpsimd.memset(w_in_planes[:].bitcast(F32), 0.0)
             make_identity(nc, ident[:])
+            nc.gpsimd.memset(w_out_planes[:].bitcast(F32), 0.0)
+            nc.vector.memset(coeff[:].bitcast(I32), 0)
 
             high_blocks = MAX_BLOCKS >> LOW_LEVELS
             for row, table in ((0, a_pad), (B_ROW, b_pad)):
@@ -111,14 +111,14 @@ def tile_butterflylayer_kernel(
                 for rows in range(half * (HALF // P), (half + 1) * (HALF // P)):
                     nc.sync.dma_start(out=x_sb[:, rows, :], in_=x[P * rows : P * (rows + 1), :])
 
+            load_x(0)
+            load_x(1)
             w_in_scale_words = w_in_scales.bitcast(I32)
             for quadrant in range(4):
                 nc.sync.dma_start(
                     out=w_in_planes[32 * quadrant : 32 * quadrant + 16, :].bitcast(I32),
                     in_=w_in_scale_words[:, 4 * quadrant : 4 * quadrant + 4, :],
                 )
-            load_x(0)
-            load_x(1)
             w_in_view = w_in_words.rearrange("g p n t -> g p (n t)").bitcast(I32).rearrange("g p n -> p g n")
             for first in range(0, FEATURES, BANK):
                 nc.sync.dma_start(out=w_in_sb[:, :, first : first + BANK], in_=w_in_view[:, :, first : first + BANK])
@@ -166,21 +166,22 @@ def tile_butterflylayer_kernel(
                 column = FEATURES - (FEATURES >> stage) + start
                 return factor[column // BANK][:, :, column % BANK : column % BANK + width]
 
-            def rotation_factors():
+            def rotation_factors(bank):
                 for stage in range(LEVELS):
                     blocks = MAX_BLOCKS >> stage
                     bit = stage if stage < LOW_LEVELS else stage - LOW_LEVELS + HIGH_BIT
                     first_column = 0 if stage < LOW_LEVELS else MAX_BLOCKS
                     width = min(blocks, BANK)
                     for start in range(0, blocks, width):
-                        for e in range(2):
-                            nc.tensor.matmul(
-                                out=factor_part(stage, start, width)[:, e, :],
-                                lhsT=pick[:, e, bit, :],
-                                rhs=coeff[:, first_column + start : first_column + start + width],
-                                start=True,
-                                stop=True,
-                            )
+                        if (FEATURES - (FEATURES >> stage) + start) // BANK == bank:
+                            for e in range(2):
+                                nc.tensor.matmul(
+                                    out=factor_part(stage, start, width)[:, e, :],
+                                    lhsT=pick[:, e, bit, :],
+                                    rhs=coeff[:, first_column + start : first_column + start + width],
+                                    start=True,
+                                    stop=True,
+                                )
 
             def rotation_products(first, end, result):
                 old = None
@@ -220,6 +221,8 @@ def tile_butterflylayer_kernel(
             def quantise_x(half):
                 grouped = []
                 for g in range(PASSES):
+                    if g % 2 == 0:
+                        rotation_factors(3 - (half * PASSES + g) // 2)
                     x_t = banks.tile([P, 2, HALF], F32, tag="bank")
                     for u in range(2):
                         for rows in range(HALF // P):
@@ -243,10 +246,8 @@ def tile_butterflylayer_kernel(
                         in_=grouped[g][:].rearrange("p b t -> p (b t)"),
                     )
 
-
             quantise_x(0)
             quantise_x(1)
-            rotation_factors()
             rotation_matrices()
             first_linear_map(0, banks)
 
@@ -301,30 +302,23 @@ def tile_butterflylayer_kernel(
             def second_linear_map(half):
                 for rows in range(HALF // P):
                     batch = slice(P * rows, P * (rows + 1))
-                    for wide in range(FEATURES // (2 * BANK)):
-                        result = late.tile([P, 2 * BANK], F32, bufs=3)
-                        for i in range(2):
-                            cols = slice(BANK * (2 * wide + i), BANK * (2 * wide + i + 1))
-                            acc = banks.tile([P, BANK], F32, tag="bank")
-                            for c in range(PASSES):
-                                nc.tensor.matmul_mx(
-                                    out=acc[:],
-                                    lhsT=h_codes[:, half, c, batch].bitcast(FP8X4),
-                                    lhsT_scale=h_planes[:, half, c, batch],
-                                    rhs=w_out_sb[:, c, cols].bitcast(FP8X4),
-                                    rhs_scale=w_out_planes[PACK * c : P, cols],
-                                    start=(c == 0),
-                                    stop=(c == PASSES - 1),
-                                )
-                            nc.vector.tensor_tensor(
-                                out=result[:, BANK * i : BANK * (i + 1)], in0=acc[:], in1=bias_sb[:, cols], op=ADD
+                    for first in range(0, FEATURES, BANK):
+                        cols = slice(first, first + BANK)
+                        acc = banks.tile([P, BANK], F32, tag="bank")
+                        for c in range(PASSES):
+                            nc.tensor.matmul_mx(
+                                out=acc[:],
+                                lhsT=h_codes[:, half, c, batch].bitcast(FP8X4),
+                                lhsT_scale=h_planes[:, half, c, batch],
+                                rhs=w_out_sb[:, c, cols].bitcast(FP8X4),
+                                rhs_scale=w_out_planes[PACK * c : P, cols],
+                                start=(c == 0),
+                                stop=(c == PASSES - 1),
                             )
+                        result = late.tile([P, BANK], F32, bufs=6)
+                        nc.vector.tensor_tensor(out=result[:], in0=acc[:], in1=bias_sb[:, cols], op=ADD)
                         nc.sync.dma_start(
-                            out=out[
-                                HALF * half + P * rows : HALF * half + P * (rows + 1),
-                                2 * BANK * wide : 2 * BANK * (wide + 1),
-                            ],
-                            in_=result[:],
+                            out=out[HALF * half + P * rows : HALF * half + P * (rows + 1), cols], in_=result[:]
                         )
 
             transpose_rotations(banks)

@@ -91,8 +91,12 @@ def tile_butterflylayer_kernel(
             x_sb = early.tile([P, BATCH // P, FEATURES], BF16)
             coeff = early.tile([P, MAX_BLOCKS + 16], BF16)
 
-            nc.gpsimd.memset(w_in_planes[:].bitcast(F32), 0.0)
+            row_number = early.tile([P, 1], I32)
+            column_number = early.tile([P, P], I32)
+            nc.gpsimd.iota(row_number[:], pattern=[[0, 1]], base=0, channel_multiplier=1)
+            nc.gpsimd.iota(column_number[:], pattern=[[1, P]], base=0, channel_multiplier=0)
             make_identity(nc, ident[:])
+            nc.gpsimd.memset(w_in_planes[:].bitcast(F32), 0.0)
             nc.gpsimd.memset(w_out_planes[:].bitcast(F32), 0.0)
             nc.vector.memset(coeff[:].bitcast(I32), 0)
 
@@ -108,8 +112,13 @@ def tile_butterflylayer_kernel(
                 )
 
             def load_x(half):
-                for rows in range(half * (HALF // P), (half + 1) * (HALF // P)):
-                    nc.sync.dma_start(out=x_sb[:, rows, :], in_=x[P * rows : P * (rows + 1), :])
+                row_blocks = slice(half * (HALF // P), (half + 1) * (HALF // P))
+                x_rows = x[HALF * half : HALF * (half + 1), :].rearrange("(r p) k -> p r k", p=P)
+                for first in range(0, FEATURES, FEATURES // 2):
+                    nc.sync.dma_start(
+                        out=x_sb[:, row_blocks, first : first + FEATURES // 2],
+                        in_=x_rows[:, :, first : first + FEATURES // 2],
+                    )
 
             load_x(0)
             load_x(1)
@@ -137,28 +146,51 @@ def tile_butterflylayer_kernel(
                 nc.sync.dma_start(out=w_out_sb[:, c, :], in_=w_out_view[c])
             nc.sync.dma_start(out=bias_sb[:], in_=b_out.partition_broadcast(P))
 
-            pick = early.tile([P, 2, LOW_LEVELS, P], BF16)
-            nc.vector.memset(pick[:].rearrange("k e l i -> k (e l i)").bitcast(I32), 0)
-            for bit in range(LOW_LEVELS):
-                for e in range(2):
-                    by_bit = pick[:, e, bit, :].rearrange("k (hi t lo) -> k hi t lo", t=2, lo=2**bit)
-                    nc.vector.memset(by_bit[0:B_ROW, :, e, :], 1.0)
-                    nc.vector.memset(by_bit[B_ROW:P, :, 1 - e, :], 2.0 * e - 1.0)
-            own_bit_f32 = early.tile([P, LOW_LEVELS], F32)
+            own_bit = early.tile([P, 1], I32)
+            nc.vector.tensor_scalar(
+                out=own_bit[:], in0=row_number[:], scalar1=HIGH_ROW - 1, scalar2=None, op0=mybir.AluOpType.bitwise_and
+            )
+            bit_of_i = early.tile([P, P], I32)
+            nc.vector.tensor_scalar(
+                out=bit_of_i[:],
+                in0=column_number[:],
+                scalar1=own_bit[:, 0:1],
+                scalar2=1,
+                op0=mybir.AluOpType.logical_shift_right,
+                op1=mybir.AluOpType.bitwise_and,
+            )
+            pick = early.tile([P, 2, P], BF16)
+            nc.vector.tensor_copy(out=pick[0:B_ROW, 1, :], in_=bit_of_i[0:B_ROW, :])
+            nc.vector.tensor_scalar(
+                out=pick[0:B_ROW, 0, :], in0=bit_of_i[0:B_ROW, :], scalar1=-1.0, scalar2=1.0, op0=MULT, op1=ADD
+            )
+            nc.vector.tensor_scalar(
+                out=pick[B_ROW:P, 1, :], in0=bit_of_i[B_ROW:P, :], scalar1=-1.0, scalar2=1.0, op0=MULT, op1=ADD
+            )
+            nc.vector.tensor_scalar(
+                out=pick[B_ROW:P, 0, :], in0=bit_of_i[B_ROW:P, :], scalar1=-1.0, scalar2=None, op0=MULT
+            )
+
+            is_own_bit = early.tile([P, LOW_LEVELS], F32)
             nc.vector.tensor_reduce(
-                out=own_bit_f32[:],
+                out=is_own_bit[:],
                 in_=ident[:].rearrange("k (q l) -> k l q", l=HIGH_ROW)[:, 0:LOW_LEVELS, :],
                 axis=mybir.AxisListType.X,
                 op=ADD,
             )
-            own_bit = early.tile([P, LOW_LEVELS], BF16)
-            nc.vector.tensor_copy(out=own_bit[:], in_=own_bit_f32[:])
-            nc.vector.tensor_tensor(
-                out=pick[:],
-                in0=pick[:],
-                in1=own_bit[:].unsqueeze(1).unsqueeze(3).to_broadcast([P, 2, LOW_LEVELS, P]),
-                op=MULT,
-            )
+            by_stage = early.tile([P, FEATURES], BF16)
+            nc.vector.memset(by_stage[:, FEATURES - 1 : FEATURES], 0.0)
+            for stage in range(LEVELS):
+                blocks = MAX_BLOCKS >> stage
+                bit = stage if stage < LOW_LEVELS else stage - LOW_LEVELS + HIGH_BIT
+                first_column = 0 if stage < LOW_LEVELS else MAX_BLOCKS
+                nc.vector.tensor_scalar(
+                    out=by_stage[:, FEATURES - 2 * blocks : FEATURES - blocks],
+                    in0=coeff[:, first_column : first_column + blocks],
+                    scalar1=is_own_bit[:, bit : bit + 1],
+                    scalar2=None,
+                    op0=MULT,
+                )
 
             factor = [tables.tile([P, 2, BANK], BF16, name="factor%d" % bank) for bank in range(4)]
 
@@ -167,21 +199,14 @@ def tile_butterflylayer_kernel(
                 return factor[column // BANK][:, :, column % BANK : column % BANK + width]
 
             def rotation_factors(bank):
-                for stage in range(LEVELS):
-                    blocks = MAX_BLOCKS >> stage
-                    bit = stage if stage < LOW_LEVELS else stage - LOW_LEVELS + HIGH_BIT
-                    first_column = 0 if stage < LOW_LEVELS else MAX_BLOCKS
-                    width = min(blocks, BANK)
-                    for start in range(0, blocks, width):
-                        if (FEATURES - (FEATURES >> stage) + start) // BANK == bank:
-                            for e in range(2):
-                                nc.tensor.matmul(
-                                    out=factor_part(stage, start, width)[:, e, :],
-                                    lhsT=pick[:, e, bit, :],
-                                    rhs=coeff[:, first_column + start : first_column + start + width],
-                                    start=True,
-                                    stop=True,
-                                )
+                for e in range(2):
+                    nc.tensor.matmul(
+                        out=factor[bank][:, e, :],
+                        lhsT=pick[:, e, :],
+                        rhs=by_stage[:, BANK * bank : BANK * (bank + 1)],
+                        start=True,
+                        stop=True,
+                    )
 
             def rotation_products(first, end, result):
                 old = None
@@ -221,8 +246,6 @@ def tile_butterflylayer_kernel(
             def quantise_x(half):
                 grouped = []
                 for g in range(PASSES):
-                    if g % 2 == 0:
-                        rotation_factors(3 - (half * PASSES + g) // 2)
                     x_t = banks.tile([P, 2, HALF], F32, tag="bank")
                     for u in range(2):
                         for rows in range(HALF // P):
@@ -233,12 +256,13 @@ def tile_butterflylayer_kernel(
                                 identity=ident[:],
                             )
                     x_grouped = early.tile([P, HALF, PACK], BF16, align_bytes=64, bufs=PASSES)
-                    copy_out(
-                        g,
-                        x_grouped[:].rearrange("p b t -> p (b t)").bitcast(F32).rearrange("p (b u) -> p b u", u=2),
-                        x_t[:].rearrange("p u b -> p b u"),
+                    nc.scalar.copy(
+                        out=x_grouped[:].rearrange("p b t -> p (b t)").bitcast(F32).rearrange("p (b u) -> p b u", u=2),
+                        in_=x_t[:].rearrange("p u b -> p b u"),
                     )
                     grouped.append(x_grouped)
+                    if g % 2 == 1:
+                        rotation_factors(3 - (half * PASSES + g) // 2)
                 for g in range(PASSES):
                     nc.vector.quantize_mx(
                         out=x_codes[:, half, g, :].bitcast(FP8X4),
@@ -282,22 +306,19 @@ def tile_butterflylayer_kernel(
 
             def high_stages(half, returned):
                 for c in range(PASSES):
-                    grouped = late.tile([P, HALF, PACK], BF16, align_bytes=64, bufs=3)
                     for rows in range(HALF // P):
+                        batch = slice(P * rows, P * (rows + 1))
                         acc = banks.tile([P, PACK, P], F32, tag="bank")
                         nc.tensor.matmul(
-                            out=acc[:],
-                            lhsT=rot_t[:, TREES, :],
-                            rhs=returned[:, c, :, P * rows : P * (rows + 1)],
-                            start=True,
-                            stop=True,
+                            out=acc[:], lhsT=rot_t[:, TREES, :], rhs=returned[:, c, :, batch], start=True, stop=True
                         )
-                        copy_out(rows, grouped[:, P * rows : P * (rows + 1), :], acc[:].rearrange("p t b -> p b t"))
-                    nc.vector.quantize_mx(
-                        out=h_codes[:, half, c, :].bitcast(FP8X4),
-                        scales=h_planes[:, half, c, :],
-                        in_=grouped[:].rearrange("p b t -> p (b t)"),
-                    )
+                        grouped = late.tile([P, P, PACK], BF16, align_bytes=64, bufs=4)
+                        copy_out(rows, grouped[:], acc[:].rearrange("p t b -> p b t"))
+                        nc.vector.quantize_mx(
+                            out=h_codes[:, half, c, batch].bitcast(FP8X4),
+                            scales=h_planes[:, half, c, batch],
+                            in_=grouped[:].rearrange("p b t -> p (b t)"),
+                        )
 
             def second_linear_map(half):
                 for rows in range(HALF // P):

@@ -10,6 +10,7 @@ U8 = mybir.dt.uint8
 FP8X4 = mybir.dt.float8_e4m3fn_x4
 MULT = mybir.AluOpType.mult
 ADD = mybir.AluOpType.add
+COPY = mybir.ActivationFunctionType.Copy
 
 P = 128
 BATCH = 512
@@ -18,7 +19,9 @@ PACK = 4
 PASSES = FEATURES // (P * PACK)
 HALVES = 2
 HALF = BATCH // HALVES
+BLOCKS = HALF // P
 TREES = FEATURES // P
+PAIRS = TREES // 2
 LEVELS = 11
 LOW_LEVELS = 7
 MAX_BLOCKS = FEATURES // 2
@@ -51,43 +54,39 @@ def tile_butterflylayer_kernel(
         w_out_planes = keep.tile([P, FEATURES], U8, align_bytes=64)
         x_codes = keep.tile([P, HALVES, PASSES, HALF], I32, align_bytes=64)
         x_planes = keep.tile([P, HALVES, PASSES, HALF], U8, align_bytes=64)
-        h_codes = keep.tile([P, HALVES, PASSES, HALF], I32, align_bytes=64)
-        h_planes = keep.tile([P, HALVES, PASSES, HALF], U8, align_bytes=64)
-        h_sb = keep.tile([P, HALVES, TREES, HALF], F32)
-        rot = keep.tile([P, TREES + 1, P], F32)
+        h_codes = keep.tile([P, HALVES, BLOCKS, PASSES, P], I32, align_bytes=64)
+        h_planes = keep.tile([P, HALVES, BLOCKS, PASSES, P], U8, align_bytes=64)
         rot_t = keep.tile([P, TREES + 1, P], F32)
         ident = keep.tile([P, P], F32)
         bias_sb = keep.tile([P, FEATURES], BF16)
 
-        def first_linear_map(half, banks):
-            for pair in range(TREES // 2):
-                acc = banks.tile([P, 2, HALF], F32, tag="bank")
-                for i in range(2):
-                    cols = slice(P * (2 * pair + i), P * (2 * pair + i + 1))
-                    for g in range(PASSES):
-                        nc.tensor.matmul_mx(
-                            out=acc[:, i, :],
-                            lhsT=w_in_sb[:, g, cols].bitcast(FP8X4),
-                            lhsT_scale=w_in_planes[PACK * g : P, cols],
-                            rhs=x_codes[:, half, g, :].bitcast(FP8X4),
-                            rhs_scale=x_planes[:, half, g, :],
-                            start=(g == 0),
-                            stop=(g == PASSES - 1),
-                        )
-                nc.scalar.copy(out=h_sb[:, half, 2 * pair : 2 * pair + 2, :], in_=acc[:])
+        high_bf = keep.tile([P, 2, LEVELS - LOW_LEVELS, 16], BF16)
+        high = keep.tile([P, 3, LEVELS - LOW_LEVELS, 16], F32)
+        h_pool = stack.enter_context(tc.tile_pool(name="h_pool", bufs=10))
+        h_pairs = {}
 
-        def transpose_rotations(banks):
-            for first in range(0, TREES + 1, 4):
-                n = min(4, TREES + 1 - first)
-                flipped = banks.tile([P, 4, P], F32, tag="bank")
-                for i in range(n):
-                    nc.tensor.transpose(out=flipped[:, i, :], in_=rot[:, first + i, :], identity=ident[:])
-                copy_out(first // 4, rot_t[:, first : first + n, :], flipped[:, 0:n, :])
-
+        def first_linear_map(half, pair, banks):
+            acc = banks.tile([P, 2, HALF], F32, tag="bank")
+            for i in range(2):
+                cols = slice(P * (2 * pair + i), P * (2 * pair + i + 1))
+                for g in range(PASSES):
+                    nc.tensor.matmul_mx(
+                        out=acc[:, i, :],
+                        lhsT=w_in_sb[:, g, cols].bitcast(FP8X4),
+                        lhsT_scale=w_in_planes[PACK * g : P, cols],
+                        rhs=x_codes[:, half, g, :].bitcast(FP8X4),
+                        rhs_scale=x_planes[:, half, g, :],
+                        start=(g == 0),
+                        stop=(g == PASSES - 1),
+                    )
+            h_pair = h_pool.tile([P, 2, HALF], F32)
+            nc.scalar.copy(out=h_pair[:], in_=acc[:])
+            h_pairs[half, pair] = h_pair
 
         with tc.tile_pool(name="early", bufs=1) as early, tc.psum_pool(name="tables", bufs=1) as tables, tc.psum_pool(
             name="first_banks", bufs=4
         ) as banks:
+            rot = early.tile([P, TREES + 1, P], F32)
             x_sb = early.tile([P, BATCH // P, FEATURES], BF16)
             coeff = early.tile([P, MAX_BLOCKS + 16], BF16)
 
@@ -120,6 +119,10 @@ def tile_butterflylayer_kernel(
                         in_=x_rows[:, :, first : first + FEATURES // 2],
                     )
 
+            for i, table in enumerate((a_pad, b_pad)):
+                nc.scalar.dma_start(
+                    out=high_bf[:, i, :, 0:high_blocks], in_=table[LOW_LEVELS:LEVELS, 0:high_blocks].partition_broadcast(P)
+                )
             load_x(0)
             load_x(1)
             w_in_scale_words = w_in_scales.bitcast(I32)
@@ -145,6 +148,16 @@ def tile_butterflylayer_kernel(
             for c in range(PASSES):
                 nc.sync.dma_start(out=w_out_sb[:, c, :], in_=w_out_view[c])
             nc.sync.dma_start(out=bias_sb[:], in_=b_out.partition_broadcast(P))
+
+            nc.gpsimd.tensor_copy(out=high[:, 0:2, :, 0:high_blocks], in_=high_bf[:, :, :, 0:high_blocks])
+            nc.gpsimd.tensor_scalar(
+                out=high[:, 2, :, 0:high_blocks],
+                in0=high_bf[:, 1, :, 0:high_blocks],
+                scalar1=-1.0,
+                scalar2=0.0,
+                op0=MULT,
+                op1=ADD,
+            )
 
             own_bit = early.tile([P, 1], I32)
             nc.vector.tensor_scalar(
@@ -270,83 +283,185 @@ def tile_butterflylayer_kernel(
                         in_=grouped[g][:].rearrange("p b t -> p (b t)"),
                     )
 
+            def transpose_rotations(banks):
+                for first in range(0, TREES + 1, 4):
+                    n = min(4, TREES + 1 - first)
+                    flipped = banks.tile([P, 4, P], F32, tag="bank")
+                    for i in range(n):
+                        nc.tensor.transpose(out=flipped[:, i, :], in_=rot[:, first + i, :], identity=ident[:])
+                    copy_out(first // 4, rot_t[:, first : first + n, :], flipped[:, 0:n, :])
+
             quantise_x(0)
             quantise_x(1)
             rotation_matrices()
-            first_linear_map(0, banks)
+            for pair in range(PAIRS):
+                first_linear_map(0, pair, banks)
+            transpose_rotations(banks)
 
         with tc.tile_pool(name="late", bufs=1, reuse_waits="tile") as late, tc.psum_pool(
             name="banks", bufs=8, reuse_waits="tile"
         ) as banks:
 
-            def low_stages(half):
-                parked = out[HALF * half : HALF * (half + 1), :].rearrange("r (f b) -> (r f) b", b=HALF)
-                for four in range(TREES // 4):
-                    low = late.tile([P, 4, HALF], F32, bufs=4)
-                    for pair in range(2):
-                        acc = banks.tile([P, 2, HALF], F32, tag="bank")
-                        for i in range(2):
-                            tree = 4 * four + 2 * pair + i
-                            nc.tensor.matmul(
-                                out=acc[:, i, :],
-                                lhsT=rot_t[:, tree, :],
-                                rhs=h_sb[:, half, tree, :],
-                                start=True,
-                                stop=True,
-                            )
-                        copy_out(pair, low[:, 2 * pair : 2 * pair + 2, :], acc[:])
+            after_7, after_8, after_9 = {}, {}, {}
+
+            def rotate(level, index, dst, src, scaled):
+                a, b, minus_b = (high[:, k, level - LOW_LEVELS, index : index + 1] for k in range(3))
+                nc.scalar.activation(out=scaled, in_=src, func=COPY, scale=a)
+                nc.vector.scalar_tensor_tensor(
+                    out=dst[:, 0], in0=src[:, 1], scalar=b, in1=scaled[:, 0], op0=MULT, op1=ADD
+                )
+                nc.vector.scalar_tensor_tensor(
+                    out=dst[:, 1], in0=src[:, 0], scalar=minus_b, in1=scaled[:, 1], op0=MULT, op1=ADD
+                )
+
+            def stage_7(half, pair, acc):
+                if pair % 2 == 0:
+                    y7 = late.tile([P, 2, 2, P], F32, bufs=3)
+                    after_7[half, pair // 2] = y7
+                scaled_7 = late.tile([P, 2, P], F32, bufs=3)
+                rotate(7, pair, after_7[half, pair // 2][:, pair % 2], acc[:, :, 0:P], scaled_7[:])
+
+            def stage_8(half, four):
+                if four % 2 == 0:
+                    y8 = late.tile([P, 2, 2, 2 * P], F32, bufs=2)
+                    after_8[half, four // 2] = y8
+                scaled_8 = late.tile([P, 2, 2 * P], F32, bufs=2)
+                src = after_7[half, four][:].rearrange("p m s b -> p m (s b)")
+                rotate(8, four, after_8[half, four // 2][:, four % 2], src, scaled_8[:])
+
+            def stage_9(half, eight):
+                if eight == 0:
+                    y9 = late.tile([P, 2, 2, 4 * P], F32)
+                    after_9[half] = y9
+                scaled_9 = late.tile([P, 2, 4 * P], F32, tag="scaled", bufs=3)
+                src = after_8[half, eight][:].rearrange("p m s b -> p m (s b)")
+                rotate(9, eight, after_9[half][:, eight], src, scaled_9[:])
+
+            def stage_10(half, part):
+                y10 = late.tile([P, 2, 4 * P], F32, bufs=3)
+                scaled_10 = late.tile([P, 2, 4 * P], F32, tag="scaled", bufs=3)
+                src = after_9[half][:, :, part, :]
+                rotate(10, 0, y10[:], src, scaled_10[:])
+                for m in range(2):
+                    first = TREES // 2 * m + 4 * part
                     nc.sync.dma_start(
-                        out=parked.rearrange("(s l) b -> l s b", l=P)[:, 4 * four : 4 * four + 4, :], in_=low[:]
+                        out=by_tree(half, 0)[:, first : first + 4, :], in_=y10[:, m].rearrange("p (s b) -> p s b", s=4)
                     )
-                returned = late.tile([P, PASSES, PACK, HALF], F32, bufs=HALVES)
-                by_pass = parked.rearrange("(h c r t) b -> c h r (t b)", h=TREES, c=PASSES, r=8, t=PACK)
+
+            def parked(half, block):
+                row = HALF * half + P * block
+                return out[row : row + P, :].rearrange("r (f b) -> (r f) b", b=P)
+
+            def by_tree(half, block):
+                return parked(half, block).rearrange("(s l) b -> l s b", l=P)
+
+            def read_back(half, block):
+                back = late.tile([P, PASSES, PACK, P], F32, bufs=3)
+                by_pass = parked(half, block).rearrange("(h c r t) b -> c h r (t b)", h=TREES, c=PASSES, r=8, t=PACK)
                 for c in range(PASSES):
-                    nc.sync.dma_start(out=returned[:, c].rearrange("p t b -> p (t b)"), in_=by_pass[c])
-                return returned
+                    nc.sync.dma_start(out=back[:, c].rearrange("p t b -> p (t b)"), in_=by_pass[c])
+                returned[half, block] = back
 
-            def high_stages(half, returned):
+            def low_stages(half, pair):
+                acc = banks.tile([P, 2, HALF], F32, tag="bank")
+                for i in range(2):
+                    nc.tensor.matmul(
+                        out=acc[:, i, :],
+                        lhsT=rot_t[:, 2 * pair + i, :],
+                        rhs=h_pairs[half, pair][:, i, :],
+                        start=True,
+                        stop=True,
+                    )
+                return acc
+
+            def group_and_quantise(half, block, c, index, src):
+                grouped = late.tile([P, P, PACK], BF16, align_bytes=64, bufs=8)
+                copy_out(index, grouped[:], src.rearrange("p t b -> p b t"))
+                return lambda: nc.vector.quantize_mx(
+                    out=h_codes[:, half, block, c, :].bitcast(FP8X4),
+                    scales=h_planes[:, half, block, c, :],
+                    in_=grouped[:].rearrange("p b t -> p (b t)"),
+                )
+
+            def high_stages(half, c):
+                acc = banks.tile([P, PACK, P], F32, tag="bank")
+                nc.tensor.matmul(
+                    out=acc[:], lhsT=rot_t[:, TREES, :], rhs=returned[half, 1][:, c], start=True, stop=True
+                )
+                return group_and_quantise(half, 1, c, c, acc[:])
+
+            def second_linear_map(half, block, n):
+                cols = slice(BANK * n, BANK * (n + 1))
+                acc = banks.tile([P, BANK], F32, tag="bank")
                 for c in range(PASSES):
-                    for rows in range(HALF // P):
-                        batch = slice(P * rows, P * (rows + 1))
-                        acc = banks.tile([P, PACK, P], F32, tag="bank")
-                        nc.tensor.matmul(
-                            out=acc[:], lhsT=rot_t[:, TREES, :], rhs=returned[:, c, :, batch], start=True, stop=True
-                        )
-                        grouped = late.tile([P, P, PACK], BF16, align_bytes=64, bufs=4)
-                        copy_out(rows, grouped[:], acc[:].rearrange("p t b -> p b t"))
-                        nc.vector.quantize_mx(
-                            out=h_codes[:, half, c, batch].bitcast(FP8X4),
-                            scales=h_planes[:, half, c, batch],
-                            in_=grouped[:].rearrange("p b t -> p (b t)"),
-                        )
+                    nc.tensor.matmul_mx(
+                        out=acc[:],
+                        lhsT=h_codes[:, half, block, c, :].bitcast(FP8X4),
+                        lhsT_scale=h_planes[:, half, block, c, :],
+                        rhs=w_out_sb[:, c, cols].bitcast(FP8X4),
+                        rhs_scale=w_out_planes[PACK * c : P, cols],
+                        start=(c == 0),
+                        stop=(c == PASSES - 1),
+                    )
+                row = HALF * half + P * block
+                result = late.tile([P, BANK], F32, bufs=6)
+                nc.vector.tensor_tensor(out=result[:], in0=acc[:], in1=bias_sb[:, cols], op=ADD)
+                nc.sync.dma_start(out=out[row : row + P, cols], in_=result[:])
 
-            def second_linear_map(half):
-                for rows in range(HALF // P):
-                    batch = slice(P * rows, P * (rows + 1))
-                    for first in range(0, FEATURES, BANK):
-                        cols = slice(first, first + BANK)
-                        acc = banks.tile([P, BANK], F32, tag="bank")
-                        for c in range(PASSES):
-                            nc.tensor.matmul_mx(
-                                out=acc[:],
-                                lhsT=h_codes[:, half, c, batch].bitcast(FP8X4),
-                                lhsT_scale=h_planes[:, half, c, batch],
-                                rhs=w_out_sb[:, c, cols].bitcast(FP8X4),
-                                rhs_scale=w_out_planes[PACK * c : P, cols],
-                                start=(c == 0),
-                                stop=(c == PASSES - 1),
-                            )
-                        result = late.tile([P, BANK], F32, bufs=6)
-                        nc.vector.tensor_tensor(out=result[:], in0=acc[:], in1=bias_sb[:, cols], op=ADD)
-                        nc.sync.dma_start(
-                            out=out[HALF * half + P * rows : HALF * half + P * (rows + 1), cols], in_=result[:]
-                        )
+            jobs = []
+            returned = {}
 
-            transpose_rotations(banks)
-            returned_0 = low_stages(0)
-            first_linear_map(1, banks)
-            returned_1 = low_stages(1)
-            high_stages(0, returned_0)
-            second_linear_map(0)
-            high_stages(1, returned_1)
-            second_linear_map(1)
+            def do_jobs(n):
+                for i in range(min(n, len(jobs))):
+                    jobs.pop(0)()
+
+            def emit(parts):
+                for part in parts:
+                    part()
+
+            def low_turn(half, pair, low):
+                acc = low_stages(half, pair)
+                stage_7(half, pair, acc)
+                copy_out(pair, low[:, 2 * (pair % 2) : 2 * (pair % 2) + 2, :], acc[:, :, P:HALF])
+                if pair % 2 == 1:
+                    nc.sync.dma_start(out=by_tree(half, 1)[:, 2 * pair - 2 : 2 * pair + 2, :], in_=low[:])
+                do_jobs(1)
+                if pair % 2 == 1:
+                    four = pair // 2
+                    jobs.append(lambda: stage_8(half, four))
+                    if four % 2 == 1:
+                        jobs.append(lambda: stage_9(half, four // 2))
+
+            def multiply_all(half, block):
+                for n in range(FEATURES // BANK):
+                    second_linear_map(half, block, n)
+
+            def all_low_stages(half):
+                for pair in range(PAIRS):
+                    if pair % 2 == 0:
+                        low = late.tile([P, 4, P], F32, bufs=4)
+                    low_turn(half, pair, low)
+                    if half == 1 and pair == 4:
+                        emit([group_and_quantise(0, 0, c, c, returned[0, 0][:, c]) for c in range(PASSES)])
+                for part in range(2):
+                    jobs.append(lambda part=part: stage_10(half, part))
+                read_back(half, 1)
+
+            all_low_stages(0)
+            for pair in range(PAIRS):
+                first_linear_map(1, pair, banks)
+                do_jobs(1)
+                if pair == 4:
+                    read_back(0, 0)
+            all_low_stages(1)
+            multiply_all(0, 0)
+            do_jobs(2)
+            parts = [high_stages(0, c) for c in range(PASSES)]
+            do_jobs(len(jobs))
+            read_back(1, 0)
+            emit(parts)
+            emit([high_stages(1, c) for c in range(PASSES)])
+            multiply_all(0, 1)
+            emit([group_and_quantise(1, 0, c, c, returned[1, 0][:, c]) for c in range(PASSES)])
+            multiply_all(1, 1)
+            multiply_all(1, 0)

@@ -80,7 +80,7 @@ def tile_butterflylayer_kernel(
                         stop=(g == PASSES - 1),
                     )
             h_pair = h_pool.tile([P, 2, HALF], F32)
-            nc.scalar.copy(out=h_pair[:], in_=acc[:])
+            copy_out(half * pair, h_pair[:], acc[:])
             h_pairs[half, pair] = h_pair
 
         with tc.tile_pool(name="early", bufs=1) as early, tc.psum_pool(name="tables", bufs=1) as tables, tc.psum_pool(
@@ -98,6 +98,8 @@ def tile_butterflylayer_kernel(
             nc.gpsimd.memset(w_in_planes[:].bitcast(F32), 0.0)
             nc.gpsimd.memset(w_out_planes[:].bitcast(F32), 0.0)
             nc.vector.memset(coeff[:].bitcast(I32), 0)
+            warm = early.tile([P, 1], F32)
+            nc.vector.memset(warm[:], 0.0)
 
             high_blocks = MAX_BLOCKS >> LOW_LEVELS
             for row, table in ((0, a_pad), (B_ROW, b_pad)):
@@ -110,6 +112,8 @@ def tile_butterflylayer_kernel(
                     in_=table[LOW_LEVELS:LEVELS, 0:high_blocks],
                 )
 
+            nc.scalar.activation(out=warm[:], in_=warm[:], func=COPY, scale=1.0)
+
             def load_x(half):
                 row_blocks = slice(half * (HALF // P), (half + 1) * (HALF // P))
                 x_rows = x[HALF * half : HALF * (half + 1), :].rearrange("(r p) k -> p r k", p=P)
@@ -119,10 +123,6 @@ def tile_butterflylayer_kernel(
                         in_=x_rows[:, :, first : first + FEATURES // 2],
                     )
 
-            for i, table in enumerate((a_pad, b_pad)):
-                nc.scalar.dma_start(
-                    out=high_bf[:, i, :, 0:high_blocks], in_=table[LOW_LEVELS:LEVELS, 0:high_blocks].partition_broadcast(P)
-                )
             load_x(0)
             load_x(1)
             w_in_scale_words = w_in_scales.bitcast(I32)
@@ -134,6 +134,10 @@ def tile_butterflylayer_kernel(
             w_in_view = w_in_words.rearrange("g p n t -> g p (n t)").bitcast(I32).rearrange("g p n -> p g n")
             for first in range(0, FEATURES, BANK):
                 nc.sync.dma_start(out=w_in_sb[:, :, first : first + BANK], in_=w_in_view[:, :, first : first + BANK])
+            for i, table in enumerate((a_pad, b_pad)):
+                nc.sync.dma_start(
+                    out=high_bf[:, i, :, 0:high_blocks], in_=table[LOW_LEVELS:LEVELS, 0:high_blocks].partition_broadcast(P)
+                )
             w_out_scale_words = w_out_scales.bitcast(I32)
             for quadrant in range(4):
                 nc.sync.dma_start(
@@ -289,7 +293,7 @@ def tile_butterflylayer_kernel(
                     flipped = banks.tile([P, 4, P], F32, tag="bank")
                     for i in range(n):
                         nc.tensor.transpose(out=flipped[:, i, :], in_=rot[:, first + i, :], identity=ident[:])
-                    copy_out(first // 4, rot_t[:, first : first + n, :], flipped[:, 0:n, :])
+                    copy_out(first // 4 + 1, rot_t[:, first : first + n, :], flipped[:, 0:n, :])
 
             quantise_x(0)
             quantise_x(1)
@@ -306,7 +310,10 @@ def tile_butterflylayer_kernel(
 
             def rotate(level, index, dst, src, scaled):
                 a, b, minus_b = (high[:, k, level - LOW_LEVELS, index : index + 1] for k in range(3))
-                nc.scalar.activation(out=scaled, in_=src, func=COPY, scale=a)
+                if level < 9:
+                    nc.scalar.activation(out=scaled, in_=src, func=COPY, scale=a)
+                else:
+                    nc.vector.tensor_scalar(out=scaled, in0=src, scalar1=a, scalar2=None, op0=MULT)
                 nc.vector.scalar_tensor_tensor(
                     out=dst[:, 0], in0=src[:, 1], scalar=b, in1=scaled[:, 0], op0=MULT, op1=ADD
                 )
@@ -388,22 +395,30 @@ def tile_butterflylayer_kernel(
                 nc.tensor.matmul(
                     out=acc[:], lhsT=rot_t[:, TREES, :], rhs=returned[half, 1][:, c], start=True, stop=True
                 )
-                return group_and_quantise(half, 1, c, c, acc[:])
+                return group_and_quantise(half, 1, c, 0, acc[:])
 
-            def second_linear_map(half, block, n):
-                cols = slice(BANK * n, BANK * (n + 1))
-                acc = banks.tile([P, BANK], F32, tag="bank")
+            def second_linear_map(half, block, columns):
+                accs = []
+                for n in columns:
+                    acc = banks.tile([P, BANK], F32, tag="bank")
+                    accs.append(acc)
                 for c in range(PASSES):
-                    nc.tensor.matmul_mx(
-                        out=acc[:],
-                        lhsT=h_codes[:, half, block, c, :].bitcast(FP8X4),
-                        lhsT_scale=h_planes[:, half, block, c, :],
-                        rhs=w_out_sb[:, c, cols].bitcast(FP8X4),
-                        rhs_scale=w_out_planes[PACK * c : P, cols],
-                        start=(c == 0),
-                        stop=(c == PASSES - 1),
-                    )
+                    for n, acc in zip(columns, accs):
+                        cols = slice(BANK * n, BANK * (n + 1))
+                        nc.tensor.matmul_mx(
+                            out=acc[:],
+                            lhsT=h_codes[:, half, block, c, :].bitcast(FP8X4),
+                            lhsT_scale=h_planes[:, half, block, c, :],
+                            rhs=w_out_sb[:, c, cols].bitcast(FP8X4),
+                            rhs_scale=w_out_planes[PACK * c : P, cols],
+                            start=(c == 0),
+                            stop=(c == PASSES - 1),
+                        )
+                return [lambda n=n, acc=acc: add_bias(half, block, n, acc) for n, acc in zip(columns, accs)]
+
+            def add_bias(half, block, n, acc):
                 row = HALF * half + P * block
+                cols = slice(BANK * n, BANK * (n + 1))
                 result = late.tile([P, BANK], F32, bufs=6)
                 nc.vector.tensor_tensor(out=result[:], in0=acc[:], in1=bias_sb[:, cols], op=ADD)
                 nc.sync.dma_start(out=out[row : row + P, cols], in_=result[:])
@@ -425,24 +440,18 @@ def tile_butterflylayer_kernel(
                 copy_out(pair, low[:, 2 * (pair % 2) : 2 * (pair % 2) + 2, :], acc[:, :, P:HALF])
                 if pair % 2 == 1:
                     nc.sync.dma_start(out=by_tree(half, 1)[:, 2 * pair - 2 : 2 * pair + 2, :], in_=low[:])
-                do_jobs(1)
+                do_jobs(pair % 2)
                 if pair % 2 == 1:
                     four = pair // 2
                     jobs.append(lambda: stage_8(half, four))
                     if four % 2 == 1:
                         jobs.append(lambda: stage_9(half, four // 2))
 
-            def multiply_all(half, block):
-                for n in range(FEATURES // BANK):
-                    second_linear_map(half, block, n)
-
             def all_low_stages(half):
                 for pair in range(PAIRS):
                     if pair % 2 == 0:
                         low = late.tile([P, 4, P], F32, bufs=4)
                     low_turn(half, pair, low)
-                    if half == 1 and pair == 4:
-                        emit([group_and_quantise(0, 0, c, c, returned[0, 0][:, c]) for c in range(PASSES)])
                 for part in range(2):
                     jobs.append(lambda part=part: stage_10(half, part))
                 read_back(half, 1)
@@ -451,17 +460,25 @@ def tile_butterflylayer_kernel(
             for pair in range(PAIRS):
                 first_linear_map(1, pair, banks)
                 do_jobs(1)
-                if pair == 4:
+                if pair == 5:
                     read_back(0, 0)
             all_low_stages(1)
-            multiply_all(0, 0)
-            do_jobs(2)
-            parts = [high_stages(0, c) for c in range(PASSES)]
+            four = range(FEATURES // BANK)
+            emit([high_stages(0, c) for c in range(PASSES)])
+            biases = second_linear_map(0, 1, four)
+            do_jobs(3)
+            emit(biases[:2])
+            do_jobs(1)
+            emit([group_and_quantise(0, 0, c, c, returned[0, 0][:, c]) for c in range(PASSES)])
+            emit(biases[2:])
             do_jobs(len(jobs))
             read_back(1, 0)
+            parts = [high_stages(1, c) for c in range(PASSES)]
+            biases = second_linear_map(0, 0, four)
             emit(parts)
-            emit([high_stages(1, c) for c in range(PASSES)])
-            multiply_all(0, 1)
+            emit(biases)
+            biases = second_linear_map(1, 1, four)
             emit([group_and_quantise(1, 0, c, c, returned[1, 0][:, c]) for c in range(PASSES)])
-            multiply_all(1, 1)
-            multiply_all(1, 0)
+            emit(biases)
+            for n in four:
+                emit(second_linear_map(1, 0, [n]))

@@ -80,7 +80,7 @@ def tile_butterflylayer_kernel(
                         stop=(g == PASSES - 1),
                     )
             h_pair = h_pool.tile([P, 2, HALF], F32)
-            copy_out(half * pair, h_pair[:], acc[:])
+            nc.scalar.copy(out=h_pair[:], in_=acc[:])
             h_pairs[half, pair] = h_pair
 
         with tc.tile_pool(name="early", bufs=1) as early, tc.psum_pool(name="tables", bufs=1) as tables, tc.psum_pool(
@@ -92,14 +92,17 @@ def tile_butterflylayer_kernel(
 
             row_number = early.tile([P, 1], I32)
             column_number = early.tile([P, P], I32)
+            nc.gpsimd.memset(coeff[:].bitcast(F32), 0.0)
             nc.gpsimd.iota(row_number[:], pattern=[[0, 1]], base=0, channel_multiplier=1)
             nc.gpsimd.iota(column_number[:], pattern=[[1, P]], base=0, channel_multiplier=0)
             make_identity(nc, ident[:])
             nc.gpsimd.memset(w_in_planes[:].bitcast(F32), 0.0)
             nc.gpsimd.memset(w_out_planes[:].bitcast(F32), 0.0)
-            nc.vector.memset(coeff[:].bitcast(I32), 0)
             warm = early.tile([P, 1], F32)
             nc.vector.memset(warm[:], 0.0)
+            filler = early.tile([P, BANK], BF16)
+            nc.vector.memset(filler[:], 0.0)
+            filler_bank = tables.tile([P, BANK], F32, name="factor0")
 
             high_blocks = MAX_BLOCKS >> LOW_LEVELS
             for row, table in ((0, a_pad), (B_ROW, b_pad)):
@@ -278,8 +281,11 @@ def tile_butterflylayer_kernel(
                         in_=x_t[:].rearrange("p u b -> p b u"),
                     )
                     grouped.append(x_grouped)
-                    if g % 2 == 1:
-                        rotation_factors(3 - (half * PASSES + g) // 2)
+                    if half == 1:
+                        rotation_factors(3 - g)
+                    elif g % 2 == 1:
+                        for i in range(2):
+                            nc.tensor.matmul(out=filler_bank[:], lhsT=filler[:, 0:P], rhs=filler[:], start=True, stop=True)
                 for g in range(PASSES):
                     nc.vector.quantize_mx(
                         out=x_codes[:, half, g, :].bitcast(FP8X4),
@@ -308,9 +314,9 @@ def tile_butterflylayer_kernel(
 
             after_7, after_8, after_9 = {}, {}, {}
 
-            def rotate(level, index, dst, src, scaled):
+            def rotate(half, level, index, dst, src, scaled):
                 a, b, minus_b = (high[:, k, level - LOW_LEVELS, index : index + 1] for k in range(3))
-                if level < 9:
+                if level < 9 or half + level == 11:
                     nc.scalar.activation(out=scaled, in_=src, func=COPY, scale=a)
                 else:
                     nc.vector.tensor_scalar(out=scaled, in0=src, scalar1=a, scalar2=None, op0=MULT)
@@ -321,12 +327,12 @@ def tile_butterflylayer_kernel(
                     out=dst[:, 1], in0=src[:, 0], scalar=minus_b, in1=scaled[:, 1], op0=MULT, op1=ADD
                 )
 
-            def stage_7(half, pair, acc):
+            def stage_7(half, pair, trees):
                 if pair % 2 == 0:
                     y7 = late.tile([P, 2, 2, P], F32, bufs=3)
                     after_7[half, pair // 2] = y7
                 scaled_7 = late.tile([P, 2, P], F32, bufs=3)
-                rotate(7, pair, after_7[half, pair // 2][:, pair % 2], acc[:, :, 0:P], scaled_7[:])
+                rotate(half, 7, pair, after_7[half, pair // 2][:, pair % 2], trees[:, :, 0:P], scaled_7[:])
 
             def stage_8(half, four):
                 if four % 2 == 0:
@@ -334,7 +340,7 @@ def tile_butterflylayer_kernel(
                     after_8[half, four // 2] = y8
                 scaled_8 = late.tile([P, 2, 2 * P], F32, bufs=2)
                 src = after_7[half, four][:].rearrange("p m s b -> p m (s b)")
-                rotate(8, four, after_8[half, four // 2][:, four % 2], src, scaled_8[:])
+                rotate(half, 8, four, after_8[half, four // 2][:, four % 2], src, scaled_8[:])
 
             def stage_9(half, eight):
                 if eight == 0:
@@ -342,13 +348,13 @@ def tile_butterflylayer_kernel(
                     after_9[half] = y9
                 scaled_9 = late.tile([P, 2, 4 * P], F32, tag="scaled", bufs=3)
                 src = after_8[half, eight][:].rearrange("p m s b -> p m (s b)")
-                rotate(9, eight, after_9[half][:, eight], src, scaled_9[:])
+                rotate(half, 9, eight, after_9[half][:, eight], src, scaled_9[:])
 
             def stage_10(half, part):
                 y10 = late.tile([P, 2, 4 * P], F32, bufs=3)
                 scaled_10 = late.tile([P, 2, 4 * P], F32, tag="scaled", bufs=3)
                 src = after_9[half][:, :, part, :]
-                rotate(10, 0, y10[:], src, scaled_10[:])
+                rotate(half, 10, 0, y10[:], src, scaled_10[:])
                 for m in range(2):
                     first = TREES // 2 * m + 4 * part
                     nc.sync.dma_start(
@@ -436,10 +442,11 @@ def tile_butterflylayer_kernel(
 
             def low_turn(half, pair, low):
                 acc = low_stages(half, pair)
-                stage_7(half, pair, acc)
-                copy_out(pair, low[:, 2 * (pair % 2) : 2 * (pair % 2) + 2, :], acc[:, :, P:HALF])
+                trees = low[:, 2 * (pair % 2) : 2 * (pair % 2) + 2, :]
+                copy_out(0, trees, acc[:])
                 if pair % 2 == 1:
-                    nc.sync.dma_start(out=by_tree(half, 1)[:, 2 * pair - 2 : 2 * pair + 2, :], in_=low[:])
+                    nc.sync.dma_start(out=by_tree(half, 1)[:, 2 * pair - 2 : 2 * pair + 2, :], in_=low[:, :, P:HALF])
+                stage_7(half, pair, trees)
                 do_jobs(pair % 2)
                 if pair % 2 == 1:
                     four = pair // 2
@@ -450,7 +457,7 @@ def tile_butterflylayer_kernel(
             def all_low_stages(half):
                 for pair in range(PAIRS):
                     if pair % 2 == 0:
-                        low = late.tile([P, 4, P], F32, bufs=4)
+                        low = late.tile([P, 4, HALF], F32, bufs=4)
                     low_turn(half, pair, low)
                 for part in range(2):
                     jobs.append(lambda part=part: stage_10(half, part))
@@ -469,7 +476,7 @@ def tile_butterflylayer_kernel(
             do_jobs(3)
             emit(biases[:2])
             do_jobs(1)
-            emit([group_and_quantise(0, 0, c, c, returned[0, 0][:, c]) for c in range(PASSES)])
+            emit([group_and_quantise(0, 0, c, 0, returned[0, 0][:, c]) for c in range(PASSES)])
             emit(biases[2:])
             do_jobs(len(jobs))
             read_back(1, 0)
@@ -478,7 +485,7 @@ def tile_butterflylayer_kernel(
             emit(parts)
             emit(biases)
             biases = second_linear_map(1, 1, four)
-            emit([group_and_quantise(1, 0, c, c, returned[1, 0][:, c]) for c in range(PASSES)])
+            emit([group_and_quantise(1, 0, c, 0, returned[1, 0][:, c]) for c in range(PASSES)])
             emit(biases)
             for n in four:
                 emit(second_linear_map(1, 0, [n]))

@@ -92,17 +92,14 @@ def tile_butterflylayer_kernel(
 
             row_number = early.tile([P, 1], I32)
             column_number = early.tile([P, P], I32)
-            nc.gpsimd.memset(coeff[:].bitcast(F32), 0.0)
             nc.gpsimd.iota(row_number[:], pattern=[[0, 1]], base=0, channel_multiplier=1)
             nc.gpsimd.iota(column_number[:], pattern=[[1, P]], base=0, channel_multiplier=0)
             make_identity(nc, ident[:])
-            nc.gpsimd.memset(w_in_planes[:].bitcast(F32), 0.0)
             nc.gpsimd.memset(w_out_planes[:].bitcast(F32), 0.0)
+            nc.vector.memset(coeff[:].bitcast(I32), 0)
+            nc.vector.memset(w_in_planes[:].bitcast(I32), 0)
             warm = early.tile([P, 1], F32)
             nc.vector.memset(warm[:], 0.0)
-            filler = early.tile([P, BANK], BF16)
-            nc.vector.memset(filler[:], 0.0)
-            filler_bank = tables.tile([P, BANK], F32, name="factor0")
 
             high_blocks = MAX_BLOCKS >> LOW_LEVELS
             for row, table in ((0, a_pad), (B_ROW, b_pad)):
@@ -115,6 +112,12 @@ def tile_butterflylayer_kernel(
                     in_=table[LOW_LEVELS:LEVELS, 0:high_blocks],
                 )
 
+            w_in_scale_words = w_in_scales.bitcast(I32)
+            for quadrant in range(4):
+                nc.scalar.dma_start(
+                    out=w_in_planes[32 * quadrant : 32 * quadrant + 16, :].bitcast(I32),
+                    in_=w_in_scale_words[:, 4 * quadrant : 4 * quadrant + 4, :],
+                )
             nc.scalar.activation(out=warm[:], in_=warm[:], func=COPY, scale=1.0)
 
             def load_x(half):
@@ -127,16 +130,11 @@ def tile_butterflylayer_kernel(
                     )
 
             load_x(0)
-            load_x(1)
-            w_in_scale_words = w_in_scales.bitcast(I32)
-            for quadrant in range(4):
-                nc.sync.dma_start(
-                    out=w_in_planes[32 * quadrant : 32 * quadrant + 16, :].bitcast(I32),
-                    in_=w_in_scale_words[:, 4 * quadrant : 4 * quadrant + 4, :],
-                )
             w_in_view = w_in_words.rearrange("g p n t -> g p (n t)").bitcast(I32).rearrange("g p n -> p g n")
             for first in range(0, FEATURES, BANK):
                 nc.sync.dma_start(out=w_in_sb[:, :, first : first + BANK], in_=w_in_view[:, :, first : first + BANK])
+                if first == 2 * BANK:
+                    load_x(1)
             for i, table in enumerate((a_pad, b_pad)):
                 nc.sync.dma_start(
                     out=high_bf[:, i, :, 0:high_blocks], in_=table[LOW_LEVELS:LEVELS, 0:high_blocks].partition_broadcast(P)
@@ -281,11 +279,9 @@ def tile_butterflylayer_kernel(
                         in_=x_t[:].rearrange("p u b -> p b u"),
                     )
                     grouped.append(x_grouped)
-                    if half == 1:
-                        rotation_factors(3 - g)
-                    elif g % 2 == 1:
-                        for i in range(2):
-                            nc.tensor.matmul(out=filler_bank[:], lhsT=filler[:, 0:P], rhs=filler[:], start=True, stop=True)
+                    if half == 0 and g == PASSES - 1:
+                        for bank in (3, 2, 1, 0):
+                            rotation_factors(bank)
                 for g in range(PASSES):
                     nc.vector.quantize_mx(
                         out=x_codes[:, half, g, :].bitcast(FP8X4),
@@ -302,10 +298,11 @@ def tile_butterflylayer_kernel(
                     copy_out(first // 4 + 1, rot_t[:, first : first + n, :], flipped[:, 0:n, :])
 
             quantise_x(0)
-            quantise_x(1)
             rotation_matrices()
             for pair in range(PAIRS):
                 first_linear_map(0, pair, banks)
+                if pair == 5:
+                    quantise_x(1)
             transpose_rotations(banks)
 
         with tc.tile_pool(name="late", bufs=1, reuse_waits="tile") as late, tc.psum_pool(

@@ -90,14 +90,20 @@ def tile_butterflylayer_kernel(
             x_sb = early.tile([P, BATCH // P, FEATURES], BF16)
             coeff = early.tile([P, MAX_BLOCKS + 16], BF16)
 
+            nc.vector.memset(coeff[:].bitcast(I32), 0)
+            nc.vector.memset(w_in_planes[:].bitcast(I32), 0)
             row_number = early.tile([P, 1], I32)
             column_number = early.tile([P, P], I32)
             nc.gpsimd.iota(row_number[:], pattern=[[0, 1]], base=0, channel_multiplier=1)
             nc.gpsimd.iota(column_number[:], pattern=[[1, P]], base=0, channel_multiplier=0)
             make_identity(nc, ident[:])
+            w_in_scale_words = w_in_scales.bitcast(I32)
+            for quadrant in range(4):
+                nc.gpsimd.dma_start(
+                    out=w_in_planes[32 * quadrant : 32 * quadrant + 16, :].bitcast(I32),
+                    in_=w_in_scale_words[:, 4 * quadrant : 4 * quadrant + 4, :],
+                )
             nc.gpsimd.memset(w_out_planes[:].bitcast(F32), 0.0)
-            nc.vector.memset(coeff[:].bitcast(I32), 0)
-            nc.vector.memset(w_in_planes[:].bitcast(I32), 0)
             warm = early.tile([P, 1], F32)
             nc.vector.memset(warm[:], 0.0)
 
@@ -112,12 +118,6 @@ def tile_butterflylayer_kernel(
                     in_=table[LOW_LEVELS:LEVELS, 0:high_blocks],
                 )
 
-            w_in_scale_words = w_in_scales.bitcast(I32)
-            for quadrant in range(4):
-                nc.scalar.dma_start(
-                    out=w_in_planes[32 * quadrant : 32 * quadrant + 16, :].bitcast(I32),
-                    in_=w_in_scale_words[:, 4 * quadrant : 4 * quadrant + 4, :],
-                )
             nc.scalar.activation(out=warm[:], in_=warm[:], func=COPY, scale=1.0)
 
             def load_x(half):
@@ -444,7 +444,7 @@ def tile_butterflylayer_kernel(
                 if pair % 2 == 1:
                     nc.sync.dma_start(out=by_tree(half, 1)[:, 2 * pair - 2 : 2 * pair + 2, :], in_=low[:, :, P:HALF])
                 stage_7(half, pair, trees)
-                do_jobs(pair % 2)
+                do_jobs(1)
                 if pair % 2 == 1:
                     four = pair // 2
                     jobs.append(lambda: stage_8(half, four))
@@ -470,16 +470,15 @@ def tile_butterflylayer_kernel(
             four = range(FEATURES // BANK)
             emit([high_stages(0, c) for c in range(PASSES)])
             biases = second_linear_map(0, 1, four)
-            do_jobs(3)
-            emit(biases[:2])
-            do_jobs(1)
+            do_jobs(2)
             emit([group_and_quantise(0, 0, c, 0, returned[0, 0][:, c]) for c in range(PASSES)])
-            emit(biases[2:])
             do_jobs(len(jobs))
             read_back(1, 0)
+            emit(biases)
             parts = [high_stages(1, c) for c in range(PASSES)]
             biases = second_linear_map(0, 0, four)
             emit(parts)
+
             emit(biases)
             biases = second_linear_map(1, 1, four)
             emit([group_and_quantise(1, 0, c, 0, returned[1, 0][:, c]) for c in range(PASSES)])

from contextlib import ExitStack

import concourse.mybir as mybir
from concourse.masks import make_identity

F32 = mybir.dt.float32
BF16 = mybir.dt.bfloat16
I32 = mybir.dt.int32
U8 = mybir.dt.uint8
FP8X4 = mybir.dt.float8_e4m3fn_x4
MULT = mybir.AluOpType.mult
ADD = mybir.AluOpType.add
COPY = mybir.ActivationFunctionType.Copy

P = 128
BATCH = 512
FEATURES = 2048
PACK = 4
PASSES = FEATURES // (P * PACK)
HALVES = 2
HALF = BATCH // HALVES
BLOCKS = HALF // P
TREES = FEATURES // P
PAIRS = TREES // 2
LEVELS = 11
LOW_LEVELS = 7
MAX_BLOCKS = FEATURES // 2
B_ROW = 64
HIGH_ROW = 32
HIGH_BIT = 3
BANK = 512

FLOPS = 2 * 2 * BATCH * FEATURES * FEATURES + 3 * LEVELS * BATCH * FEATURES


def tile_butterflylayer_kernel(
    tc, x, w_in_words, w_in_scales, w_out_words, w_out_scales, b_out, a_pad, b_pad, out
):
    nc = tc.nc

    def copy_out(index, dst, src):
        if index % 2 == 0:
            nc.scalar.copy(out=dst, in_=src)
        else:
            nc.vector.tensor_copy(out=dst, in_=src)

    with ExitStack() as stack:
        stack.enter_context(tc.manual_schedule())
        keep = stack.enter_context(tc.tile_pool(name="keep", bufs=1))

        w_in_sb = keep.tile([P, PASSES, FEATURES], I32, align_bytes=64)
        w_out_sb = keep.tile([P, PASSES, FEATURES], I32, align_bytes=64)
        w_in_planes = keep.tile([P, FEATURES], U8, align_bytes=64)
        w_out_planes = keep.tile([P, FEATURES], U8, align_bytes=64)
        x_codes = keep.tile([P, HALVES, PASSES, HALF], I32, align_bytes=64)
        x_planes = keep.tile([P, HALVES, PASSES, HALF], U8, align_bytes=64)
        h_codes = keep.tile([P, HALVES, BLOCKS, PASSES, P], I32, align_bytes=64)
        h_planes = keep.tile([P, HALVES, BLOCKS, PASSES, P], U8, align_bytes=64)
        rot_t = keep.tile([P, TREES + 1, P], F32)
        ident = keep.tile([P, P], F32)
        bias_sb = keep.tile([P, FEATURES], BF16)

        high_bf = keep.tile([P, 2, LEVELS - LOW_LEVELS, 16], BF16)
        high = keep.tile([P, 3, LEVELS - LOW_LEVELS, 16], F32)
        h_pool = stack.enter_context(tc.tile_pool(name="h_pool", bufs=10))
        h_pairs = {}

        def first_linear_map(half, pair, banks):
            acc = banks.tile([P, 2, HALF], F32, tag="bank")
            for i in range(2):
                cols = slice(P * (2 * pair + i), P * (2 * pair + i + 1))
                for g in range(PASSES):
                    nc.tensor.matmul_mx(
                        out=acc[:, i, :],
                        lhsT=w_in_sb[:, g, cols].bitcast(FP8X4),
                        lhsT_scale=w_in_planes[PACK * g : P, cols],
                        rhs=x_codes[:, half, g, :].bitcast(FP8X4),
                        rhs_scale=x_planes[:, half, g, :],
                        start=(g == 0),
                        stop=(g == PASSES - 1),
                    )
            h_pair = h_pool.tile([P, 2, HALF], F32)
            nc.scalar.copy(out=h_pair[:], in_=acc[:])
            h_pairs[half, pair] = h_pair

        with tc.tile_pool(name="early", bufs=1) as early, tc.psum_pool(name="tables", bufs=1) as tables, tc.psum_pool(
            name="first_banks", bufs=4
        ) as banks:
            rot = early.tile([P, TREES + 1, P], F32)
            x_sb = early.tile([P, BATCH // P, FEATURES], BF16)
            coeff = early.tile([P, MAX_BLOCKS + 16], BF16)

            nc.vector.memset(coeff[:].bitcast(I32), 0)
            nc.vector.memset(w_in_planes[:].bitcast(I32), 0)
            row_number = early.tile([P, 1], I32)
            column_number = early.tile([P, P], I32)
            nc.gpsimd.iota(row_number[:], pattern=[[0, 1]], base=0, channel_multiplier=1)
            nc.gpsimd.iota(column_number[:], pattern=[[1, P]], base=0, channel_multiplier=0)
            make_identity(nc, ident[:])
            w_in_scale_words = w_in_scales.bitcast(I32)
            for quadrant in range(4):
                nc.gpsimd.dma_start(
                    out=w_in_planes[32 * quadrant : 32 * quadrant + 16, :].bitcast(I32),
                    in_=w_in_scale_words[:, 4 * quadrant : 4 * quadrant + 4, :],
                )
            nc.gpsimd.memset(w_out_planes[:].bitcast(F32), 0.0)
            warm = early.tile([P, 1], F32)
            nc.vector.memset(warm[:], 0.0)

            high_blocks = MAX_BLOCKS >> LOW_LEVELS
            for row, table in ((0, a_pad), (B_ROW, b_pad)):
                nc.scalar.dma_start(out=coeff[row : row + LOW_LEVELS, 0:MAX_BLOCKS], in_=table[0:LOW_LEVELS, :])
                nc.scalar.dma_start(
                    out=coeff[
                        row + HIGH_ROW + HIGH_BIT : row + HIGH_ROW + HIGH_BIT + LEVELS - LOW_LEVELS,
                        MAX_BLOCKS : MAX_BLOCKS + high_blocks,
                    ],
                    in_=table[LOW_LEVELS:LEVELS, 0:high_blocks],
                )

            nc.scalar.activation(out=warm[:], in_=warm[:], func=COPY, scale=1.0)

            def load_x(half):
                row_blocks = slice(half * (HALF // P), (half + 1) * (HALF // P))
                x_rows = x[HALF * half : HALF * (half + 1), :].rearrange("(r p) k -> p r k", p=P)
                for first in range(0, FEATURES, FEATURES // 2):
                    nc.sync.dma_start(
                        out=x_sb[:, row_blocks, first : first + FEATURES // 2],
                        in_=x_rows[:, :, first : first + FEATURES // 2],
                    )

            load_x(0)
            w_in_view = w_in_words.rearrange("g p n t -> g p (n t)").bitcast(I32).rearrange("g p n -> p g n")
            for first in range(0, FEATURES, BANK):
                nc.sync.dma_start(out=w_in_sb[:, :, first : first + BANK], in_=w_in_view[:, :, first : first + BANK])
                if first == 2 * BANK:
                    load_x(1)
            for i, table in enumerate((a_pad, b_pad)):
                nc.sync.dma_start(
                    out=high_bf[:, i, :, 0:high_blocks], in_=table[LOW_LEVELS:LEVELS, 0:high_blocks].partition_broadcast(P)
                )
            w_out_scale_words = w_out_scales.bitcast(I32)
            for quadrant in range(4):
                nc.sync.dma_start(
                    out=w_out_planes[32 * quadrant : 32 * quadrant + 16, :].bitcast(I32),
                    in_=w_out_scale_words[quadrant].rearrange("(h c) n -> c h n", c=PASSES),
                )
            w_out_view = (
                w_out_words.rearrange("g p n t -> g p (n t)")
                .bitcast(I32)
                .rearrange("g (h c r) n -> c (g h) r n", h=4, c=PASSES, r=8)
            )
            for c in range(PASSES):
                nc.sync.dma_start(out=w_out_sb[:, c, :], in_=w_out_view[c])
            nc.sync.dma_start(out=bias_sb[:], in_=b_out.partition_broadcast(P))

            nc.gpsimd.tensor_copy(out=high[:, 0:2, :, 0:high_blocks], in_=high_bf[:, :, :, 0:high_blocks])
            nc.gpsimd.tensor_scalar(
                out=high[:, 2, :, 0:high_blocks],
                in0=high_bf[:, 1, :, 0:high_blocks],
                scalar1=-1.0,
                scalar2=0.0,
                op0=MULT,
                op1=ADD,
            )

            own_bit = early.tile([P, 1], I32)
            nc.vector.tensor_scalar(
                out=own_bit[:], in0=row_number[:], scalar1=HIGH_ROW - 1, scalar2=None, op0=mybir.AluOpType.bitwise_and
            )
            bit_of_i = early.tile([P, P], I32)
            nc.vector.tensor_scalar(
                out=bit_of_i[:],
                in0=column_number[:],
                scalar1=own_bit[:, 0:1],
                scalar2=1,
                op0=mybir.AluOpType.logical_shift_right,
                op1=mybir.AluOpType.bitwise_and,
            )
            pick = early.tile([P, 2, P], BF16)
            nc.vector.tensor_copy(out=pick[0:B_ROW, 1, :], in_=bit_of_i[0:B_ROW, :])
            nc.vector.tensor_scalar(
                out=pick[0:B_ROW, 0, :], in0=bit_of_i[0:B_ROW, :], scalar1=-1.0, scalar2=1.0, op0=MULT, op1=ADD
            )
            nc.vector.tensor_scalar(
                out=pick[B_ROW:P, 1, :], in0=bit_of_i[B_ROW:P, :], scalar1=-1.0, scalar2=1.0, op0=MULT, op1=ADD
            )
            nc.vector.tensor_scalar(
                out=pick[B_ROW:P, 0, :], in0=bit_of_i[B_ROW:P, :], scalar1=-1.0, scalar2=None, op0=MULT
            )

            is_own_bit = early.tile([P, LOW_LEVELS], F32)
            nc.vector.tensor_reduce(
                out=is_own_bit[:],
                in_=ident[:].rearrange("k (q l) -> k l q", l=HIGH_ROW)[:, 0:LOW_LEVELS, :],
                axis=mybir.AxisListType.X,
                op=ADD,
            )
            by_stage = early.tile([P, FEATURES], BF16)
            nc.vector.memset(by_stage[:, FEATURES - 1 : FEATURES], 0.0)
            for stage in range(LEVELS):
                blocks = MAX_BLOCKS >> stage
                bit = stage if stage < LOW_LEVELS else stage - LOW_LEVELS + HIGH_BIT
                first_column = 0 if stage < LOW_LEVELS else MAX_BLOCKS
                nc.vector.tensor_scalar(
                    out=by_stage[:, FEATURES - 2 * blocks : FEATURES - blocks],
                    in0=coeff[:, first_column : first_column + blocks],
                    scalar1=is_own_bit[:, bit : bit + 1],
                    scalar2=None,
                    op0=MULT,
                )

            factor = [tables.tile([P, 2, BANK], BF16, name="factor%d" % bank) for bank in range(4)]

            def factor_part(stage, start, width):
                column = FEATURES - (FEATURES >> stage) + start
                return factor[column // BANK][:, :, column % BANK : column % BANK + width]

            def rotation_factors(bank):
                for e in range(2):
                    nc.tensor.matmul(
                        out=factor[bank][:, e, :],
                        lhsT=pick[:, e, :],
                        rhs=by_stage[:, BANK * bank : BANK * (bank + 1)],
                        start=True,
                        stop=True,
                    )

            def rotation_products(first, end, result):
                old = None
                for stage in reversed(range(first, end)):
                    blocks = MAX_BLOCKS >> stage
                    new = result if stage == first else early.tile([P, 2 * blocks], F32, name="product%d" % stage)
                    width = min(blocks, BANK)
                    for start in range(0, blocks, width):
                        new_part = new[:, 2 * start : 2 * (start + width)].rearrange("p (b e) -> p b e", e=2)
                        by_block = factor_part(stage, start, width).rearrange("p e b -> p b e")
                        if old is None:
                            nc.vector.tensor_copy(out=new_part, in_=by_block)
                        else:
                            nc.vector.tensor_tensor(
                                out=new_part,
                                in0=old[:, start : start + width].unsqueeze(2).to_broadcast([P, width, 2]),
                                in1=by_block,
                                op=MULT,
                            )
                    old = new

            def rotation_matrices():
                rotation_products(0, LOW_LEVELS, rot[:, 0:TREES, :].rearrange("p s j -> p (s j)"))
                high = early.tile([P, TREES], F32)
                rotation_products(LOW_LEVELS, LEVELS, high[:])
                same_r = early.tile([P, 8], F32)
                nc.vector.tensor_reduce(
                    out=same_r[:], in_=ident[:].rearrange("p (h r) -> p r h", r=8), axis=mybir.AxisListType.X, op=ADD
                )
                nc.vector.tensor_tensor(
                    out=rot[:, TREES, :].rearrange("p (h r) -> p h r", r=8),
                    in0=high[:].unsqueeze(2).to_broadcast([P, TREES, 8]),
                    in1=same_r[:].unsqueeze(1).to_broadcast([P, TREES, 8]),
                    op=MULT,
                )

            def quantise_x(half):
                grouped = []
                for g in range(PASSES):
                    x_t = banks.tile([P, 2, HALF], F32, tag="bank")
                    for u in range(2):
                        for rows in range(HALF // P):
                            x_words = x_sb[:, half * (HALF // P) + rows, :].bitcast(F32)
                            nc.tensor.transpose(
                                out=x_t[:, u, P * rows : P * (rows + 1)],
                                in_=x_words[:, 256 * g + u : 256 * (g + 1) : 2],
                                identity=ident[:],
                            )
                    x_grouped = early.tile([P, HALF, PACK], BF16, align_bytes=64, bufs=PASSES)
                    nc.scalar.copy(
                        out=x_grouped[:].rearrange("p b t -> p (b t)").bitcast(F32).rearrange("p (b u) -> p b u", u=2),
                        in_=x_t[:].rearrange("p u b -> p b u"),
                    )
                    grouped.append(x_grouped)
                    if half == 0 and g == PASSES - 1:
                        for bank in (3, 2, 1, 0):
                            rotation_factors(bank)
                for g in range(PASSES):
                    nc.vector.quantize_mx(
                        out=x_codes[:, half, g, :].bitcast(FP8X4),
                        scales=x_planes[:, half, g, :],
                        in_=grouped[g][:].rearrange("p b t -> p (b t)"),
                    )

            def transpose_rotations(banks):
                for first in range(0, TREES + 1, 4):
                    n = min(4, TREES + 1 - first)
                    flipped = banks.tile([P, 4, P], F32, tag="bank")
                    for i in range(n):
                        nc.tensor.transpose(out=flipped[:, i, :], in_=rot[:, first + i, :], identity=ident[:])
                    copy_out(first // 4 + 1, rot_t[:, first : first + n, :], flipped[:, 0:n, :])

            quantise_x(0)
            rotation_matrices()
            for pair in range(PAIRS):
                first_linear_map(0, pair, banks)
                if pair == 5:
                    quantise_x(1)
            transpose_rotations(banks)

        with tc.tile_pool(name="late", bufs=1, reuse_waits="tile") as late, tc.psum_pool(
            name="banks", bufs=8, reuse_waits="tile"
        ) as banks:

            after_7, after_8, after_9 = {}, {}, {}

            def rotate(half, level, index, dst, src, scaled):
                a, b, minus_b = (high[:, k, level - LOW_LEVELS, index : index + 1] for k in range(3))
                if level < 9 or half + level == 11:
                    nc.scalar.activation(out=scaled, in_=src, func=COPY, scale=a)
                else:
                    nc.vector.tensor_scalar(out=scaled, in0=src, scalar1=a, scalar2=None, op0=MULT)
                nc.vector.scalar_tensor_tensor(
                    out=dst[:, 0], in0=src[:, 1], scalar=b, in1=scaled[:, 0], op0=MULT, op1=ADD
                )
                nc.vector.scalar_tensor_tensor(
                    out=dst[:, 1], in0=src[:, 0], scalar=minus_b, in1=scaled[:, 1], op0=MULT, op1=ADD
                )

            def stage_7(half, pair, trees):
                if pair % 2 == 0:
                    y7 = late.tile([P, 2, 2, P], F32, bufs=3)
                    after_7[half, pair // 2] = y7
                scaled_7 = late.tile([P, 2, P], F32, bufs=3)
                rotate(half, 7, pair, after_7[half, pair // 2][:, pair % 2], trees[:, :, 0:P], scaled_7[:])

            def stage_8(half, four):
                if four % 2 == 0:
                    y8 = late.tile([P, 2, 2, 2 * P], F32, bufs=2)
                    after_8[half, four // 2] = y8
                scaled_8 = late.tile([P, 2, 2 * P], F32, bufs=2)
                src = after_7[half, four][:].rearrange("p m s b -> p m (s b)")
                rotate(half, 8, four, after_8[half, four // 2][:, four % 2], src, scaled_8[:])

            def stage_9(half, eight):
                if eight == 0:
                    y9 = late.tile([P, 2, 2, 4 * P], F32)
                    after_9[half] = y9
                scaled_9 = late.tile([P, 2, 4 * P], F32, tag="scaled", bufs=3)
                src = after_8[half, eight][:].rearrange("p m s b -> p m (s b)")
                rotate(half, 9, eight, after_9[half][:, eight], src, scaled_9[:])

            def stage_10(half, part):
                y10 = late.tile([P, 2, 4 * P], F32, bufs=3)
                scaled_10 = late.tile([P, 2, 4 * P], F32, tag="scaled", bufs=3)
                src = after_9[half][:, :, part, :]
                rotate(half, 10, 0, y10[:], src, scaled_10[:])
                for m in range(2):
                    first = TREES // 2 * m + 4 * part
                    nc.sync.dma_start(
                        out=by_tree(half, 0)[:, first : first + 4, :], in_=y10[:, m].rearrange("p (s b) -> p s b", s=4)
                    )

            def parked(half, block):
                row = HALF * half + P * block
                return out[row : row + P, :].rearrange("r (f b) -> (r f) b", b=P)

            def by_tree(half, block):
                return parked(half, block).rearrange("(s l) b -> l s b", l=P)

            def read_back(half, block):
                back = late.tile([P, PASSES, PACK, P], F32, bufs=3)
                by_pass = parked(half, block).rearrange("(h c r t) b -> c h r (t b)", h=TREES, c=PASSES, r=8, t=PACK)
                for c in range(PASSES):
                    nc.sync.dma_start(out=back[:, c].rearrange("p t b -> p (t b)"), in_=by_pass[c])
                returned[half, block] = back

            def low_stages(half, pair):
                acc = banks.tile([P, 2, HALF], F32, tag="bank")
                for i in range(2):
                    nc.tensor.matmul(
                        out=acc[:, i, :],
                        lhsT=rot_t[:, 2 * pair + i, :],
                        rhs=h_pairs[half, pair][:, i, :],
                        start=True,
                        stop=True,
                    )
                return acc

            def group_and_quantise(half, block, c, index, src):
                grouped = late.tile([P, P, PACK], BF16, align_bytes=64, bufs=8)
                copy_out(index, grouped[:], src.rearrange("p t b -> p b t"))
                return lambda: nc.vector.quantize_mx(
                    out=h_codes[:, half, block, c, :].bitcast(FP8X4),
                    scales=h_planes[:, half, block, c, :],
                    in_=grouped[:].rearrange("p b t -> p (b t)"),
                )

            def high_stages(half, c):
                acc = banks.tile([P, PACK, P], F32, tag="bank")
                nc.tensor.matmul(
                    out=acc[:], lhsT=rot_t[:, TREES, :], rhs=returned[half, 1][:, c], start=True, stop=True
                )
                return group_and_quantise(half, 1, c, 0, acc[:])

            def second_linear_map(half, block, columns):
                accs = []
                for n in columns:
                    acc = banks.tile([P, BANK], F32, tag="bank")
                    accs.append(acc)
                for c in range(PASSES):
                    for n, acc in zip(columns, accs):
                        cols = slice(BANK * n, BANK * (n + 1))
                        nc.tensor.matmul_mx(
                            out=acc[:],
                            lhsT=h_codes[:, half, block, c, :].bitcast(FP8X4),
                            lhsT_scale=h_planes[:, half, block, c, :],
                            rhs=w_out_sb[:, c, cols].bitcast(FP8X4),
                            rhs_scale=w_out_planes[PACK * c : P, cols],
                            start=(c == 0),
                            stop=(c == PASSES - 1),
                        )
                return [lambda n=n, acc=acc: add_bias(half, block, n, acc) for n, acc in zip(columns, accs)]

            def add_bias(half, block, n, acc):
                row = HALF * half + P * block
                cols = slice(BANK * n, BANK * (n + 1))
                result = late.tile([P, BANK], F32, bufs=6)
                nc.vector.tensor_tensor(out=result[:], in0=acc[:], in1=bias_sb[:, cols], op=ADD)
                nc.sync.dma_start(out=out[row : row + P, cols], in_=result[:])

            jobs = []
            returned = {}

            def do_jobs(n):
                for i in range(min(n, len(jobs))):
                    jobs.pop(0)()

            def emit(parts):
                for part in parts:
                    part()

            def low_turn(half, pair, low):
                acc = low_stages(half, pair)
                trees = low[:, 2 * (pair % 2) : 2 * (pair % 2) + 2, :]
                copy_out(0, trees, acc[:])
                if pair % 2 == 1:
                    nc.sync.dma_start(out=by_tree(half, 1)[:, 2 * pair - 2 : 2 * pair + 2, :], in_=low[:, :, P:HALF])
                stage_7(half, pair, trees)
                do_jobs(1)
                if pair % 2 == 1:
                    four = pair // 2
                    jobs.append(lambda: stage_8(half, four))
                    if four % 2 == 1:
                        jobs.append(lambda: stage_9(half, four // 2))

            def all_low_stages(half):
                for pair in range(PAIRS):
                    if pair % 2 == 0:
                        low = late.tile([P, 4, HALF], F32, bufs=4)
                    low_turn(half, pair, low)
                for part in range(2):
                    jobs.append(lambda part=part: stage_10(half, part))
                read_back(half, 1)

            all_low_stages(0)
            for pair in range(PAIRS):
                first_linear_map(1, pair, banks)
                do_jobs(1)
                if pair == 5:
                    read_back(0, 0)
            all_low_stages(1)
            four = range(FEATURES // BANK)
            emit([high_stages(0, c) for c in range(PASSES)])
            biases = second_linear_map(0, 1, four)
            do_jobs(2)
            emit([group_and_quantise(0, 0, c, 0, returned[0, 0][:, c]) for c in range(PASSES)])
            do_jobs(len(jobs))
            read_back(1, 0)
            emit(biases)
            parts = [high_stages(1, c) for c in range(PASSES)]
            biases = second_linear_map(0, 0, four)
            emit(parts)

            emit(biases)
            biases = second_linear_map(1, 1, four)
            emit([group_and_quantise(1, 0, c, 0, returned[1, 0][:, c]) for c in range(PASSES)])
            emit(biases)
            for n in four:
                emit(second_linear_map(1, 0, [n]))
